import numpy as np
import ml_dtypes


def mxq(x, axis, fmt="e4m3"):
    dtype, down = {"e4m3": (ml_dtypes.float8_e4m3fn, 7), "e5m2": (ml_dtypes.float8_e5m2, 14)}[fmt]
    v = np.moveaxis(np.asarray(x, np.float32).astype(ml_dtypes.bfloat16).astype(np.float64), axis, -1)
    blocks = v.reshape(v.shape[:-1] + (-1, 32))
    amax = np.abs(blocks).max(-1, keepdims=True)
    byte = np.maximum(np.where(amax > 0, np.frexp(amax)[1] - 1 + 127, 0) - down, 1)
    scale = np.exp2(byte - 127.0)
    codes = (blocks / scale).astype(np.float32).astype(dtype).astype(np.float64)
    return np.moveaxis((codes * scale).reshape(v.shape), -1, axis)


WIDE = False


def mx_kscale(k):
    if not WIDE:
        return np.ones(k)
    levels = np.array([10, -10, 5, -5, 0])
    a = np.random.permutation(np.resize(levels, k // 512 * 4)).reshape(k // 512, 4)
    idx = np.arange(k)
    return np.exp2(a[idx // 512, idx % 128 // 32])


BF16 = ml_dtypes.bfloat16


def bf(x):
    return np.asarray(x, np.float32).astype(BF16)


def f64(x):
    return np.asarray(x).astype(np.float64)


NU, NI, NE, EMB = 1536, 2560, 1024, 512
N = NU + NI
LN_EPS = 1e-5
DENS = 0.01
A_SCALE = (1.5e-4 / ((NE * DENS) ** 2 + N * NE * DENS ** 2 * (1.0 + NE * DENS ** 2))) ** 0.25


def setup_inputs():
    s = mx_kscale(N)
    adj = (np.random.uniform(size=(N, NE)) < DENS) * np.random.uniform(0.5, 1.5, (N, NE)) * A_SCALE
    return {"e_nodes": bf(np.random.standard_normal((N, EMB)) / s[:, None]),
            "adj": bf(adj * s[:, None]),
            "ego_embeddings": bf(np.random.standard_normal((N, EMB))),
            "ln_gamma": bf(1.0 + 0.1 * np.random.standard_normal(EMB)),
            "ln_beta": bf(0.1 * np.random.standard_normal(EMB))}


def reference(e_nodes, adj, ego_embeddings, ln_gamma, ln_beta):
    a = f64(adj)
    m = mxq(a.T, 1, "e4m3") @ mxq(f64(e_nodes), 0, "e4m3")
    h = mxq(a, 1, "e4m3") @ mxq(m, 0, "e4m3")
    mu = h.mean(-1, keepdims=True)
    var = h.var(-1, keepdims=True)
    return (h - mu) * (1.0 / np.sqrt(var + LN_EPS)) * f64(ln_gamma) + f64(ln_beta) + f64(ego_embeddings)

@@ -1,0 +1,268 @@
+from contextlib import ExitStack
+
+import concourse.mybir as mybir
+from concourse.masks import make_identity
+
+BF16 = mybir.dt.bfloat16
+F32 = mybir.dt.float32
+U32 = mybir.dt.uint32
+U8 = mybir.dt.uint8
+FP8X4 = mybir.dt.float8_e4m3fn_x4
+ALU = mybir.AluOpType
+ACT = mybir.ActivationFunctionType
+
+P = 128
+PACK = 4
+K_PASS = P * PACK
+NODES, EDGES, EMB = 4096, 1024, 512
+GROUPS = NODES // K_PASS
+EDGE_PASSES = EDGES // K_PASS
+EDGE_TILES = EDGES // P
+QUARTERS = EDGES // (2 * P)
+LN_EPS = 1e-5
+LOAD_AHEAD = 3
+LEAD = 2
+
+FLOPS = 2 * 2 * NODES * EDGES * EMB
+
+
+def tile_hgnnmodel_pa_t_kernel(tc, e_nodes, adj, ego_embeddings, ln_gamma, ln_beta, out):
+    nc = tc.nc
+
+    def node_rows(dram, g):
+        return dram[g * K_PASS : (g + 1) * K_PASS, :].rearrange("(p j) c -> p (j c)", j=PACK)
+
+    with ExitStack() as ctx:
+        ctx.enter_context(tc.manual_schedule())
+        consts = ctx.enter_context(tc.tile_pool(name="consts", bufs=1))
+        resident = ctx.enter_context(tc.tile_pool(name="resident", bufs=1))
+        results = ctx.enter_context(tc.tile_pool(name="results", bufs=3))
+        psum = ctx.enter_context(tc.psum_pool(name="psum", bufs=8))
+
+        identity = consts.tile([P, P], F32)
+        make_identity(nc, identity[:])
+
+        ones = consts.tile([P, P], BF16)
+        nc.vector.memset(ones[:], 1.0)
+        table_warmer = consts.tile([P, 1], F32)
+        nc.scalar.sqrt(out=table_warmer[:], in_=ones[:, 0:1])
+        vector_rows = consts.tile([P, 2 * EMB], BF16)
+        nc.vector.memset(vector_rows[:], 0.0)
+        nc.scalar.dma_start(out=vector_rows[0:1, 0:EMB], in_=ln_gamma.unsqueeze(0))
+        nc.scalar.dma_start(out=vector_rows[0:1, EMB : 2 * EMB], in_=ln_beta.unsqueeze(0))
+        gamma_all = consts.tile([P, EMB], F32)
+        beta_all = consts.tile([P, EMB], F32)
+        for i, spread in enumerate((gamma_all, beta_all)):
+            spread_bank = psum.tile([P, EMB], F32, tag="bank")
+            nc.tensor.matmul(
+                out=spread_bank[:],
+                lhsT=ones[:],
+                rhs=vector_rows[:, i * EMB : (i + 1) * EMB],
+                start=True,
+                stop=True,
+            )
+            nc.scalar.copy(out=spread[:], in_=spread_bank[:])
+
+        adj_rows = []
+        e_rows = []
+        adj_grouped = []
+        e_grouped = []
+        m_banks = [psum.tile([P, EMB], F32, tag="bank", name="m_bank%d" % t) for t in range(EDGE_TILES)]
+        m_bf16 = resident.tile([P, EDGE_TILES, EMB], BF16)
+
+        with tc.tile_pool(name="stage1_rows", bufs=LOAD_AHEAD + 1) as rows_pool, tc.tile_pool(
+            name="stage1", bufs=3
+        ) as stage1:
+
+            def load_group(g):
+                adj_tile = resident.tile([P, PACK * EDGES], BF16, name="adj_rows%d" % g)
+                nc.sync.dma_start(out=adj_tile[:], in_=node_rows(adj, g))
+                adj_rows.append(adj_tile)
+                e_tile = rows_pool.tile([P, PACK * EMB], BF16, name="e_rows")
+                nc.sync.dma_start(out=e_tile[:], in_=node_rows(e_nodes, g))
+                e_rows.append(e_tile)
+
+            def regroup(g):
+                adj_tile = stage1.tile([P, EDGES, PACK], BF16, align_bytes=64, name="adj_grouped")
+                dst = adj_tile[:].rearrange("p (a s q) j -> p s a q j", a=QUARTERS, s=2, q=P)
+                src = adj_rows[g][:].rearrange("p (j a q s) -> p s a q j", j=PACK, a=QUARTERS, q=P, s=2)
+                e_tile = stage1.tile([P, EMB, PACK], BF16, align_bytes=64, name="e_grouped")
+                nc.scalar.copy(
+                    out=e_tile[:].rearrange("p (c i) j -> p c j i", i=4),
+                    in_=e_rows[g][:].rearrange("p (j c i) -> p c j i", j=PACK, i=4),
+                )
+                nc.vector.tensor_copy(out=dst[:, :, 0 : QUARTERS - 1], in_=src[:, :, 0 : QUARTERS - 1])
+                nc.scalar.copy(out=dst[:, :, QUARTERS - 1], in_=src[:, :, QUARTERS - 1])
+                adj_grouped.append(adj_tile)
+                e_grouped.append(e_tile)
+
+            def quantise_and_multiply(g):
+                adj_codes = stage1.tile([P, EDGES], U32, align_bytes=64)
+                adj_scales = stage1.tile([P, EDGES], U8, align_bytes=64)
+                nc.vector.quantize_mx(
+                    out=adj_codes[:].bitcast(FP8X4),
+                    scales=adj_scales[:],
+                    in_=adj_grouped[g][:].rearrange("p w j -> p (w j)"),
+                )
+                e_codes = stage1.tile([P, EMB], U32, align_bytes=64)
+                e_scales = stage1.tile([P, EMB], U8, align_bytes=64)
+                nc.vector.quantize_mx(
+                    out=e_codes[:].bitcast(FP8X4),
+                    scales=e_scales[:],
+                    in_=e_grouped[g][:].rearrange("p w j -> p (w j)"),
+                )
+                for t in range(EDGE_TILES):
+                    nc.tensor.matmul_mx(
+                        out=m_banks[t][:],
+                        lhsT=adj_codes[:, t * P : (t + 1) * P].bitcast(FP8X4),
+                        lhsT_scale=adj_scales[:, t * P : (t + 1) * P],
+                        rhs=e_codes[:].bitcast(FP8X4),
+                        rhs_scale=e_scales[:],
+                        start=(g == 0),
+                        stop=(g == GROUPS - 1),
+                    )
+
+            for g in range(LOAD_AHEAD):
+                load_group(g)
+            for g in range(GROUPS):
+                if g + LOAD_AHEAD < GROUPS:
+                    load_group(g + LOAD_AHEAD)
+                regroup(g)
+                if g > 0:
+                    quantise_and_multiply(g - 1)
+            quantise_and_multiply(GROUPS - 1)
+
+            ego_rows = []
+            for g in range(GROUPS):
+                ego_tile = resident.tile([P, PACK, EMB], BF16, name="ego_rows%d" % g)
+                nc.sync.dma_start(
+                    out=ego_tile[:].rearrange("p j f -> p (j f)"), in_=node_rows(ego_embeddings, g)
+                )
+                ego_rows.append(ego_tile)
+
+        for t in range(EDGE_TILES):
+            if t % 2 == 0:
+                nc.scalar.copy(out=m_bf16[:, t, :], in_=m_banks[t][:])
+            else:
+                nc.vector.tensor_copy(out=m_bf16[:, t, :], in_=m_banks[t][:])
+        m_grouped = resident.tile([P, EDGE_PASSES, EMB, PACK], BF16, align_bytes=64)
+        m_codes = resident.tile([P, EDGE_PASSES, EMB], U32, align_bytes=64)
+        m_scales = resident.tile([P, EDGE_PASSES, EMB], U8, align_bytes=64)
+        for k in range(EDGE_PASSES):
+            nc.vector.tensor_copy(
+                out=m_grouped[:, k].rearrange("p (c i) t -> p c t i", i=4),
+                in_=m_bf16[:, k * PACK : (k + 1) * PACK, :].rearrange("p t (c i) -> p c t i", i=4),
+            )
+        for k in range(EDGE_PASSES):
+            nc.vector.quantize_mx(
+                out=m_codes[:, k, :].bitcast(FP8X4),
+                scales=m_scales[:, k, :],
+                in_=m_grouped[:, k].rearrange("p f t -> p (f t)"),
+            )
+
+        stage2 = ctx.enter_context(tc.tile_pool(name="stage2", bufs=2))
+        codes_pool = ctx.enter_context(tc.tile_pool(name="stage2_codes", bufs=LEAD + 1))
+        adjT_codes = []
+        adjT_scales = []
+
+        def transpose_and_quantise(g):
+            grouped = stage2.tile([P, EDGE_PASSES * PACK * P * PACK], BF16, align_bytes=64, name="adjT_grouped")
+            grouped_words = grouped[:].bitcast(F32).rearrange(
+                "p (k j r u) -> p k j r u", k=EDGE_PASSES, j=PACK, r=P, u=2
+            )
+            words = adj_rows[g][:].bitcast(F32)
+            row_words = EDGES // 2
+            for j in range(PACK):
+                transposed = psum.tile([P, 2 * EDGE_PASSES, P], F32, tag="bank")
+                for c in range(2 * EDGE_PASSES):
+                    nc.tensor.transpose(
+                        transposed[:, c, :],
+                        words[:, j * row_words + c * P : j * row_words + (c + 1) * P],
+                        identity[:],
+                    )
+                nc.scalar.copy(
+                    out=grouped_words[:, :, j],
+                    in_=transposed[:].rearrange("p (k u) r -> p k r u", u=2),
+                )
+            codes = codes_pool.tile([P, EDGE_PASSES * PACK * P], U32, align_bytes=64, name="adjT_codes")
+            scales = codes_pool.tile([P, EDGE_PASSES * PACK * P], U8, align_bytes=64, name="adjT_scales")
+            nc.vector.quantize_mx(out=codes[:].bitcast(FP8X4), scales=scales[:], in_=grouped[:])
+            adjT_codes.append(codes)
+            adjT_scales.append(scales)
+
+        for g in range(LEAD):
+            transpose_and_quantise(g)
+
+        for g in range(GROUPS):
+            h_banks = []
+            for j in range(PACK):
+                h_bank = psum.tile([P, EMB], F32, tag="bank")
+                for k in range(EDGE_PASSES):
+                    cols = slice((k * PACK + j) * P, (k * PACK + j + 1) * P)
+                    nc.tensor.matmul_mx(
+                        out=h_bank[:],
+                        lhsT=adjT_codes[g][:, cols].bitcast(FP8X4),
+                        lhsT_scale=adjT_scales[g][:, cols],
+                        rhs=m_codes[:, k, :].bitcast(FP8X4),
+                        rhs_scale=m_scales[:, k, :],
+                        start=(k == 0),
+                        stop=(k == EDGE_PASSES - 1),
+                    )
+                h_banks.append(h_bank)
+
+            result = results.tile([P, PACK, EMB], F32)
+            nc.vector.tensor_tensor(
+                out=result[:],
+                in0=ego_rows[g][:],
+                in1=beta_all[:].unsqueeze(1).to_broadcast([P, PACK, EMB]),
+                op=ALU.add,
+            )
+
+            h = stage2.tile([P, PACK, EMB], F32)
+            row_sum = stage2.tile([P, PACK], F32)
+            for j in range(PACK):
+                nc.scalar.activation(
+                    out=h[:, j, :], in_=h_banks[j][:], func=ACT.Identity, accum_out=row_sum[:, j : j + 1]
+                )
+            neg_mean = stage2.tile([P, PACK], F32)
+            nc.scalar.mul(out=neg_mean[:], in_=row_sum[:], mul=-1.0 / EMB)
+
+            centred = stage2.tile([P, PACK, EMB], F32)
+            for j in range(PACK):
+                nc.vector.scalar_tensor_tensor(
+                    out=centred[:, j, :],
+                    in0=h[:, j, :],
+                    scalar=neg_mean[:, j : j + 1],
+                    in1=gamma_all[:],
+                    op0=ALU.add,
+                    op1=ALU.mult,
+                )
+
+            if g + LEAD < GROUPS:
+                transpose_and_quantise(g + LEAD)
+
+            square_sum = stage2.tile([P, PACK], F32)
+            for j in range(PACK):
+                squares = stage2.tile([P, EMB], BF16)
+                nc.scalar.activation(
+                    out=squares[:],
+                    in_=h[:, j, :],
+                    func=ACT.Square,
+                    bias=neg_mean[:, j : j + 1],
+                    accum_out=square_sum[:, j : j + 1],
+                )
+            std = stage2.tile([P, PACK], F32)
+            nc.scalar.activation(out=std[:], in_=square_sum[:], func=ACT.Sqrt, bias=LN_EPS, scale=1.0 / EMB)
+            rstd = stage2.tile([P, PACK], F32)
+            nc.vector.reciprocal(out=rstd[:], in_=std[:])
+
+            for j in range(PACK):
+                nc.vector.scalar_tensor_tensor(
+                    out=result[:, j, :],
+                    in0=centred[:, j, :],
+                    scalar=rstd[:, j : j + 1],
+                    in1=result[:, j, :],
+                    op0=ALU.mult,
+                    op1=ALU.add,
+                )
+            nc.sync.dma_start(out=node_rows(out, g), in_=result[:].rearrange("p j f -> p (j f)"))

@@ -36,7 +36,7 @@ def tile_hgnnmodel_pa_t_kernel(tc, e_nodes, adj, ego_embeddings, ln_gamma, ln_be
         ctx.enter_context(tc.manual_schedule())
         consts = ctx.enter_context(tc.tile_pool(name="consts", bufs=1))
         resident = ctx.enter_context(tc.tile_pool(name="resident", bufs=1))
-        results = ctx.enter_context(tc.tile_pool(name="results", bufs=3))
+        results = ctx.enter_context(tc.tile_pool(name="results", bufs=LEAD + 2))
         psum = ctx.enter_context(tc.psum_pool(name="psum", bufs=8))
 
         identity = consts.tile([P, P], F32)
@@ -48,8 +48,8 @@ def tile_hgnnmodel_pa_t_kernel(tc, e_nodes, adj, ego_embeddings, ln_gamma, ln_be
         nc.scalar.sqrt(out=table_warmer[:], in_=ones[:, 0:1])
         vector_rows = consts.tile([P, 2 * EMB], BF16)
         nc.vector.memset(vector_rows[:], 0.0)
-        nc.scalar.dma_start(out=vector_rows[0:1, 0:EMB], in_=ln_gamma.unsqueeze(0))
-        nc.scalar.dma_start(out=vector_rows[0:1, EMB : 2 * EMB], in_=ln_beta.unsqueeze(0))
+        nc.sync.dma_start(out=vector_rows[0:1, 0:EMB], in_=ln_gamma.unsqueeze(0))
+        nc.sync.dma_start(out=vector_rows[0:1, EMB : 2 * EMB], in_=ln_beta.unsqueeze(0))
         gamma_all = consts.tile([P, EMB], F32)
         beta_all = consts.tile([P, EMB], F32)
         for i, spread in enumerate((gamma_all, beta_all)):
@@ -72,7 +72,7 @@ def tile_hgnnmodel_pa_t_kernel(tc, e_nodes, adj, ego_embeddings, ln_gamma, ln_be
 
         with tc.tile_pool(name="stage1_rows", bufs=LOAD_AHEAD + 1) as rows_pool, tc.tile_pool(
             name="stage1", bufs=3
-        ) as stage1:
+        ) as stage1, tc.tile_pool(name="stage1_codes", bufs=2) as stage1_codes:
 
             def load_group(g):
                 adj_tile = resident.tile([P, PACK * EDGES], BF16, name="adj_rows%d" % g)
@@ -97,15 +97,15 @@ def tile_hgnnmodel_pa_t_kernel(tc, e_nodes, adj, ego_embeddings, ln_gamma, ln_be
                 e_grouped.append(e_tile)
 
             def quantise_and_multiply(g):
-                adj_codes = stage1.tile([P, EDGES], U32, align_bytes=64)
-                adj_scales = stage1.tile([P, EDGES], U8, align_bytes=64)
+                adj_codes = stage1_codes.tile([P, EDGES], U32, align_bytes=64)
+                adj_scales = stage1_codes.tile([P, EDGES], U8, align_bytes=64)
                 nc.vector.quantize_mx(
                     out=adj_codes[:].bitcast(FP8X4),
                     scales=adj_scales[:],
                     in_=adj_grouped[g][:].rearrange("p w j -> p (w j)"),
                 )
-                e_codes = stage1.tile([P, EMB], U32, align_bytes=64)
-                e_scales = stage1.tile([P, EMB], U8, align_bytes=64)
+                e_codes = stage1_codes.tile([P, EMB], U32, align_bytes=64)
+                e_scales = stage1_codes.tile([P, EMB], U8, align_bytes=64)
                 nc.vector.quantize_mx(
                     out=e_codes[:].bitcast(FP8X4),
                     scales=e_scales[:],
@@ -140,11 +140,22 @@ def tile_hgnnmodel_pa_t_kernel(tc, e_nodes, adj, ego_embeddings, ln_gamma, ln_be
                 )
                 ego_rows.append(ego_tile)
 
+        result_tiles = []
+
+        def residual(g):
+            result = results.tile([P, PACK, EMB], F32)
+            nc.vector.tensor_tensor(
+                out=result[:],
+                in0=ego_rows[g][:],
+                in1=beta_all[:].unsqueeze(1).to_broadcast([P, PACK, EMB]),
+                op=ALU.add,
+            )
+            result_tiles.append(result)
+
+        for g in range(LEAD):
+            residual(g)
         for t in range(EDGE_TILES):
-            if t % 2 == 0:
-                nc.scalar.copy(out=m_bf16[:, t, :], in_=m_banks[t][:])
-            else:
-                nc.vector.tensor_copy(out=m_bf16[:, t, :], in_=m_banks[t][:])
+            nc.scalar.copy(out=m_bf16[:, t, :], in_=m_banks[t][:])
         m_grouped = resident.tile([P, EDGE_PASSES, EMB, PACK], BF16, align_bytes=64)
         m_codes = resident.tile([P, EDGE_PASSES, EMB], U32, align_bytes=64)
         m_scales = resident.tile([P, EDGE_PASSES, EMB], U8, align_bytes=64)
@@ -210,13 +221,8 @@ def tile_hgnnmodel_pa_t_kernel(tc, e_nodes, adj, ego_embeddings, ln_gamma, ln_be
                     )
                 h_banks.append(h_bank)
 
-            result = results.tile([P, PACK, EMB], F32)
-            nc.vector.tensor_tensor(
-                out=result[:],
-                in0=ego_rows[g][:],
-                in1=beta_all[:].unsqueeze(1).to_broadcast([P, PACK, EMB]),
-                op=ALU.add,
-            )
+            if g + LEAD < GROUPS:
+                residual(g + LEAD)
 
             h = stage2.tile([P, PACK, EMB], F32)
             row_sum = stage2.tile([P, PACK], F32)
@@ -256,6 +262,7 @@ def tile_hgnnmodel_pa_t_kernel(tc, e_nodes, adj, ego_embeddings, ln_gamma, ln_be
             rstd = stage2.tile([P, PACK], F32)
             nc.vector.reciprocal(out=rstd[:], in_=std[:])
 
+            result = result_tiles[g]
             for j in range(PACK):
                 nc.vector.scalar_tensor_tensor(
                     out=result[:, j, :],
@@ -265,4 +272,4 @@ def tile_hgnnmodel_pa_t_kernel(tc, e_nodes, adj, ego_embeddings, ln_gamma, ln_be
                     op0=ALU.mult,
                     op1=ALU.add,
                 )
-            nc.sync.dma_start(out=node_rows(out, g), in_=result[:].rearrange("p j f -> p (j f)"))
+                nc.sync.dma_start(out=node_rows(out, g)[:, j * EMB : (j + 1) * EMB], in_=result[:, j, :])

@@ -84,15 +84,17 @@ def tile_hgnnmodel_pa_t_kernel(tc, e_nodes, adj, ego_embeddings, ln_gamma, ln_be
 
             def regroup(g):
                 adj_tile = stage1.tile([P, EDGES, PACK], BF16, align_bytes=64, name="adj_grouped")
-                dst = adj_tile[:].rearrange("p (a s q) j -> p s a q j", a=QUARTERS, s=2, q=P)
-                src = adj_rows[g][:].rearrange("p (j a q s) -> p s a q j", j=PACK, a=QUARTERS, q=P, s=2)
+                dst = adj_tile[:].rearrange("p (a s c i) j -> p s a c j i", a=QUARTERS, s=2, i=4)
+                src = adj_rows[g][:].rearrange("p (j a c i s) -> p s a c j i", j=PACK, a=QUARTERS, i=4, s=2)
                 e_tile = stage1.tile([P, EMB, PACK], BF16, align_bytes=64, name="e_grouped")
                 nc.scalar.copy(
                     out=e_tile[:].rearrange("p (c i) j -> p c j i", i=4),
                     in_=e_rows[g][:].rearrange("p (j c i) -> p c j i", j=PACK, i=4),
                 )
-                nc.vector.tensor_copy(out=dst[:, :, 0 : QUARTERS - 1], in_=src[:, :, 0 : QUARTERS - 1])
-                nc.scalar.copy(out=dst[:, :, QUARTERS - 1], in_=src[:, :, QUARTERS - 1])
+                nc.vector.tensor_copy(out=dst[:, 0], in_=src[:, 0])
+                nc.vector.tensor_copy(out=dst[:, 1, 0 : QUARTERS // 2], in_=src[:, 1, 0 : QUARTERS // 2])
+                for a in range(QUARTERS // 2, QUARTERS):
+                    nc.scalar.copy(out=dst[:, 1, a], in_=src[:, 1, a])
                 adj_grouped.append(adj_tile)
                 e_grouped.append(e_tile)
 

@@ -21,7 +21,9 @@ EDGE_TILES = EDGES // P
 QUARTERS = EDGES // (2 * P)
 LN_EPS = 1e-5
 LOAD_AHEAD = 3
-LEAD = 2
+PAIR = 2
+PAIRS = NODES // (PAIR * P)
+LEAD = 4
 
 FLOPS = 2 * 2 * NODES * EDGES * EMB
 
@@ -36,11 +38,17 @@ def tile_hgnnmodel_pa_t_kernel(tc, e_nodes, adj, ego_embeddings, ln_gamma, ln_be
         ctx.enter_context(tc.manual_schedule())
         consts = ctx.enter_context(tc.tile_pool(name="consts", bufs=1))
         resident = ctx.enter_context(tc.tile_pool(name="resident", bufs=1))
-        results = ctx.enter_context(tc.tile_pool(name="results", bufs=LEAD + 2))
-        psum = ctx.enter_context(tc.psum_pool(name="psum", bufs=8))
+        results = ctx.enter_context(tc.tile_pool(name="results", bufs=4))
+        psum = ctx.enter_context(tc.psum_pool(name="psum", bufs=1))
+        tag_banks = {"sums": 3, "turned": 2, "residual": 3}
+
+        def bank(tag, name="bank"):
+            return psum.tile([P, EMB], F32, tag=tag, bufs=tag_banks[tag], name=name)
 
         identity = consts.tile([P, P], F32)
         make_identity(nc, identity[:])
+        identity_bf16 = consts.tile([P, P], BF16)
+        nc.gpsimd.tensor_copy(out=identity_bf16[:], in_=identity[:])
 
         ones = consts.tile([P, P], BF16)
         nc.vector.memset(ones[:], 1.0)
@@ -48,26 +56,12 @@ def tile_hgnnmodel_pa_t_kernel(tc, e_nodes, adj, ego_embeddings, ln_gamma, ln_be
         nc.scalar.sqrt(out=table_warmer[:], in_=ones[:, 0:1])
         vector_rows = consts.tile([P, 2 * EMB], BF16)
         nc.vector.memset(vector_rows[:], 0.0)
-        nc.sync.dma_start(out=vector_rows[0:1, 0:EMB], in_=ln_gamma.unsqueeze(0))
-        nc.sync.dma_start(out=vector_rows[0:1, EMB : 2 * EMB], in_=ln_beta.unsqueeze(0))
-        gamma_all = consts.tile([P, EMB], F32)
-        beta_all = consts.tile([P, EMB], F32)
-        for i, spread in enumerate((gamma_all, beta_all)):
-            spread_bank = psum.tile([P, EMB], F32, tag="bank")
-            nc.tensor.matmul(
-                out=spread_bank[:],
-                lhsT=ones[:],
-                rhs=vector_rows[:, i * EMB : (i + 1) * EMB],
-                start=True,
-                stop=True,
-            )
-            nc.scalar.copy(out=spread[:], in_=spread_bank[:])
-
+        nc.scalar.dma_start(out=vector_rows[0:1, 0:EMB], in_=ln_gamma.unsqueeze(0))
+        nc.scalar.dma_start(out=vector_rows[0:1, EMB : 2 * EMB], in_=ln_beta.unsqueeze(0))
         adj_rows = []
         e_rows = []
         adj_grouped = []
         e_grouped = []
-        m_banks = [psum.tile([P, EMB], F32, tag="bank", name="m_bank%d" % t) for t in range(EDGE_TILES)]
         m_bf16 = resident.tile([P, EDGE_TILES, EMB], BF16)
 
         with tc.tile_pool(name="stage1_rows", bufs=LOAD_AHEAD + 1) as rows_pool, tc.tile_pool(
@@ -75,12 +69,18 @@ def tile_hgnnmodel_pa_t_kernel(tc, e_nodes, adj, ego_embeddings, ln_gamma, ln_be
         ) as stage1, tc.tile_pool(name="stage1_codes", bufs=2) as stage1_codes:
 
             def load_group(g):
-                adj_tile = resident.tile([P, PACK * EDGES], BF16, name="adj_rows%d" % g)
-                nc.sync.dma_start(out=adj_tile[:], in_=node_rows(adj, g))
-                adj_rows.append(adj_tile)
                 e_tile = rows_pool.tile([P, PACK * EMB], BF16, name="e_rows")
                 nc.sync.dma_start(out=e_tile[:], in_=node_rows(e_nodes, g))
                 e_rows.append(e_tile)
+                adj_tile = resident.tile([P, PACK * EDGES], BF16, name="adj_rows%d" % g)
+                pieces = 2 if g == 0 else 1
+                for h in range(pieces):
+                    cols = slice(h * EDGES // pieces, (h + 1) * EDGES // pieces)
+                    nc.sync.dma_start(
+                        out=adj_tile[:].rearrange("p (j c) -> p j c", j=PACK)[:, :, cols],
+                        in_=node_rows(adj, g).rearrange("p (j c) -> p j c", j=PACK)[:, :, cols],
+                    )
+                adj_rows.append(adj_tile)
 
             def regroup(g):
                 adj_tile = stage1.tile([P, EDGES, PACK], BF16, align_bytes=64, name="adj_grouped")
@@ -91,8 +91,9 @@ def tile_hgnnmodel_pa_t_kernel(tc, e_nodes, adj, ego_embeddings, ln_gamma, ln_be
                     out=e_tile[:].rearrange("p (c i) j -> p c j i", i=4),
                     in_=e_rows[g][:].rearrange("p (j c i) -> p c j i", j=PACK, i=4),
                 )
-                nc.vector.tensor_copy(out=dst[:, 0], in_=src[:, 0])
-                nc.vector.tensor_copy(out=dst[:, 1, 0 : QUARTERS // 2], in_=src[:, 1, 0 : QUARTERS // 2])
+                for s in range(2):
+                    nc.vector.tensor_copy(out=dst[:, s, 0 : QUARTERS // 2], in_=src[:, s, 0 : QUARTERS // 2])
+                nc.vector.tensor_copy(out=dst[:, 0, QUARTERS // 2 :], in_=src[:, 0, QUARTERS // 2 :])
                 for a in range(QUARTERS // 2, QUARTERS):
                     nc.scalar.copy(out=dst[:, 1, a], in_=src[:, 1, a])
                 adj_grouped.append(adj_tile)
@@ -126,10 +127,27 @@ def tile_hgnnmodel_pa_t_kernel(tc, e_nodes, adj, ego_embeddings, ln_gamma, ln_be
 
             for g in range(LOAD_AHEAD):
                 load_group(g)
+            for g in range(2):
+                regroup(g)
+            gamma_all = consts.tile([P, EMB], F32)
+            beta_all = consts.tile([P, EMB], F32)
+            for i, spread in enumerate((gamma_all, beta_all)):
+                spread_bank = bank("sums")
+                nc.tensor.matmul(
+                    out=spread_bank[:],
+                    lhsT=ones[:],
+                    rhs=vector_rows[:, i * EMB : (i + 1) * EMB],
+                    start=True,
+                    stop=True,
+                )
+                nc.scalar.copy(out=spread[:], in_=spread_bank[:])
+            m_tags = ("turned", "turned", "sums", "sums", "sums", "residual", "residual", "residual")
+            m_banks = [bank(m_tags[t], name="m_bank%d" % t) for t in range(EDGE_TILES)]
             for g in range(GROUPS):
                 if g + LOAD_AHEAD < GROUPS:
                     load_group(g + LOAD_AHEAD)
-                regroup(g)
+                if g > 1:
+                    regroup(g)
                 if g > 0:
                     quantise_and_multiply(g - 1)
             quantise_and_multiply(GROUPS - 1)
@@ -142,80 +160,131 @@ def tile_hgnnmodel_pa_t_kernel(tc, e_nodes, adj, ego_embeddings, ln_gamma, ln_be
                 )
                 ego_rows.append(ego_tile)
 
-        result_tiles = []
+        stage2 = ctx.enter_context(tc.tile_pool(name="stage2", bufs=3))
+        codes_pool = ctx.enter_context(tc.tile_pool(name="stage2_codes", bufs=LEAD + 1))
+        turned_words = []
+        adjT_codes = []
+        adjT_scales = []
 
-        def residual(g):
-            result = results.tile([P, PACK, EMB], F32)
-            nc.vector.tensor_tensor(
-                out=result[:],
-                in0=ego_rows[g][:],
-                in1=beta_all[:].unsqueeze(1).to_broadcast([P, PACK, EMB]),
-                op=ALU.add,
+        def transpose(s):
+            grouped = stage2.tile([P, EDGE_PASSES * PAIR * P * PACK], BF16, align_bytes=64, name="adjT_grouped")
+            grouped_words = grouped[:].bitcast(F32).rearrange(
+                "p (k j r u) -> p k j r u", k=EDGE_PASSES, j=PAIR, r=P, u=2
             )
-            result_tiles.append(result)
+            row_words = EDGES // 2
+            words = adj_rows[s * PAIR // PACK][:].bitcast(F32)
+            for i in range(PAIR):
+                j = (s * PAIR + i) % PACK
+                turned = bank("turned")
+                for c in range(2 * EDGE_PASSES):
+                    nc.tensor.transpose(
+                        turned[:, c * P : (c + 1) * P],
+                        words[:, j * row_words + c * P : j * row_words + (c + 1) * P],
+                        identity[:],
+                    )
+                nc.scalar.copy(
+                    out=grouped_words[:, :, i],
+                    in_=turned[:].rearrange("p (k u r) -> p k r u", k=EDGE_PASSES, u=2),
+                )
+            turned_words.append(grouped)
 
-        for g in range(LEAD):
-            residual(g)
-        for t in range(EDGE_TILES):
-            nc.scalar.copy(out=m_bf16[:, t, :], in_=m_banks[t][:])
+        def quantise_turned(s):
+            codes = codes_pool.tile([P, EDGE_PASSES * PAIR * P], U32, align_bytes=64, name="adjT_codes")
+            scales = codes_pool.tile([P, EDGE_PASSES * PAIR * P], U8, align_bytes=64, name="adjT_scales")
+            nc.vector.quantize_mx(out=codes[:].bitcast(FP8X4), scales=scales[:], in_=turned_words[s][:])
+            adjT_codes.append(codes)
+            adjT_scales.append(scales)
+
         m_grouped = resident.tile([P, EDGE_PASSES, EMB, PACK], BF16, align_bytes=64)
         m_codes = resident.tile([P, EDGE_PASSES, EMB], U32, align_bytes=64)
         m_scales = resident.tile([P, EDGE_PASSES, EMB], U8, align_bytes=64)
-        for k in range(EDGE_PASSES):
+
+        def empty_m_bank(t):
+            copy = nc.vector.tensor_copy if t % 2 else nc.scalar.copy
+            copy(out=m_bf16[:, t, :], in_=m_banks[t][:])
+
+        def regroup_m(k):
             nc.vector.tensor_copy(
                 out=m_grouped[:, k].rearrange("p (c i) t -> p c t i", i=4),
                 in_=m_bf16[:, k * PACK : (k + 1) * PACK, :].rearrange("p t (c i) -> p c t i", i=4),
             )
-        for k in range(EDGE_PASSES):
+
+        def quantise_m(k):
             nc.vector.quantize_mx(
                 out=m_codes[:, k, :].bitcast(FP8X4),
                 scales=m_scales[:, k, :],
                 in_=m_grouped[:, k].rearrange("p f t -> p (f t)"),
             )
 
-        stage2 = ctx.enter_context(tc.tile_pool(name="stage2", bufs=2))
-        codes_pool = ctx.enter_context(tc.tile_pool(name="stage2_codes", bufs=LEAD + 1))
-        adjT_codes = []
-        adjT_scales = []
+        for t in range(PACK):
+            empty_m_bank(t)
+        regroup_m(0)
+        for t in range(PACK, EDGE_TILES):
+            empty_m_bank(t)
+        quantise_m(0)
+        regroup_m(1)
+        transpose(0)
+        quantise_turned(0)
+        quantise_m(1)
+        for s in range(1, LEAD):
+            transpose(s)
+            quantise_turned(s)
 
-        def transpose_and_quantise(g):
-            grouped = stage2.tile([P, EDGE_PASSES * PACK * P * PACK], BF16, align_bytes=64, name="adjT_grouped")
-            grouped_words = grouped[:].bitcast(F32).rearrange(
-                "p (k j r u) -> p k j r u", k=EDGE_PASSES, j=PACK, r=P, u=2
-            )
-            words = adj_rows[g][:].bitcast(F32)
-            row_words = EDGES // 2
-            for j in range(PACK):
-                transposed = psum.tile([P, 2 * EDGE_PASSES, P], F32, tag="bank")
-                for c in range(2 * EDGE_PASSES):
-                    nc.tensor.transpose(
-                        transposed[:, c, :],
-                        words[:, j * row_words + c * P : j * row_words + (c + 1) * P],
-                        identity[:],
+        VECTOR_RESIDUAL = PACK - 1
+
+        def residual(s):
+            tiles = []
+            for i in range(PAIR):
+                g, j = divmod(s * PAIR + i, PACK)
+                if j == VECTOR_RESIDUAL:
+                    tile = stage2.tile([P, EMB], F32, name="vector_residual")
+                    nc.vector.tensor_tensor(
+                        out=tile[:], in0=ego_rows[g][:, j, :], in1=beta_all[:], op=ALU.add
                     )
-                nc.scalar.copy(
-                    out=grouped_words[:, :, j],
-                    in_=transposed[:].rearrange("p (k u) r -> p k r u", u=2),
+                else:
+                    tile = bank("residual")
+                    nc.tensor.matmul(
+                        out=tile[:], lhsT=identity_bf16[:], rhs=ego_rows[g][:, j, :], start=True, stop=False
+                    )
+                    nc.tensor.matmul(
+                        out=tile[:], lhsT=ones[:], rhs=vector_rows[:, EMB : 2 * EMB], start=False, stop=True
+                    )
+                tiles.append(tile)
+            return tiles
+
+        def on_vector(s, i):
+            return (s * PAIR + i) % 8 == 1
+
+        def invert(std):
+            rstd = stage2.tile([P, PAIR], F32)
+            nc.vector.reciprocal(out=rstd[:], in_=std[:])
+            return rstd
+
+        def finish(s, residuals, centred, rstd):
+            for i in range(PAIR):
+                g, j = divmod(s * PAIR + i, PACK)
+                result = results.tile([P, EMB], F32)
+                nc.vector.scalar_tensor_tensor(
+                    out=result[:],
+                    in0=centred[:, i, :],
+                    scalar=rstd[:, i : i + 1],
+                    in1=residuals[i][:],
+                    op0=ALU.mult,
+                    op1=ALU.add,
                 )
-            codes = codes_pool.tile([P, EDGE_PASSES * PACK * P], U32, align_bytes=64, name="adjT_codes")
-            scales = codes_pool.tile([P, EDGE_PASSES * PACK * P], U8, align_bytes=64, name="adjT_scales")
-            nc.vector.quantize_mx(out=codes[:].bitcast(FP8X4), scales=scales[:], in_=grouped[:])
-            adjT_codes.append(codes)
-            adjT_scales.append(scales)
+                nc.sync.dma_start(out=node_rows(out, g)[:, j * EMB : (j + 1) * EMB], in_=result[:])
 
-        for g in range(LEAD):
-            transpose_and_quantise(g)
-
-        for g in range(GROUPS):
+        waiting = None
+        for s in range(PAIRS):
             h_banks = []
-            for j in range(PACK):
-                h_bank = psum.tile([P, EMB], F32, tag="bank")
+            for i in range(PAIR):
+                h_bank = bank("sums")
                 for k in range(EDGE_PASSES):
-                    cols = slice((k * PACK + j) * P, (k * PACK + j + 1) * P)
+                    cols = slice((k * PAIR + i) * P, (k * PAIR + i + 1) * P)
                     nc.tensor.matmul_mx(
                         out=h_bank[:],
-                        lhsT=adjT_codes[g][:, cols].bitcast(FP8X4),
-                        lhsT_scale=adjT_scales[g][:, cols],
+                        lhsT=adjT_codes[s][:, cols].bitcast(FP8X4),
+                        lhsT_scale=adjT_scales[s][:, cols],
                         rhs=m_codes[:, k, :].bitcast(FP8X4),
                         rhs_scale=m_scales[:, k, :],
                         start=(k == 0),
@@ -223,55 +292,64 @@ def tile_hgnnmodel_pa_t_kernel(tc, e_nodes, adj, ego_embeddings, ln_gamma, ln_be
                     )
                 h_banks.append(h_bank)
 
-            if g + LEAD < GROUPS:
-                residual(g + LEAD)
+            if waiting is not None:
+                rstd_before = invert(waiting[3])
 
-            h = stage2.tile([P, PACK, EMB], F32)
-            row_sum = stage2.tile([P, PACK], F32)
-            for j in range(PACK):
-                nc.scalar.activation(
-                    out=h[:, j, :], in_=h_banks[j][:], func=ACT.Identity, accum_out=row_sum[:, j : j + 1]
-                )
-            neg_mean = stage2.tile([P, PACK], F32)
-            nc.scalar.mul(out=neg_mean[:], in_=row_sum[:], mul=-1.0 / EMB)
+            h = stage2.tile([P, PAIR, EMB], F32)
+            row_sum = stage2.tile([P, PAIR], F32)
+            mean = stage2.tile([P, PAIR], F32)
+            stats = stage2.tile([P, 6], F32)
+            moments = stage2.tile([P, 2], F32)
+            for i in range(PAIR):
+                if on_vector(s, i):
+                    nc.vector.bn_stats(out=stats[:], in_=h_banks[i][:])
+                else:
+                    nc.scalar.activation(
+                        out=h[:, i, :], in_=h_banks[i][:], func=ACT.Identity, accum_out=row_sum[:, i : i + 1]
+                    )
+            on_scalar = slice(0, 1) if on_vector(s, 1) else slice(0, PAIR)
+            nc.scalar.mul(out=mean[:, on_scalar], in_=row_sum[:, on_scalar], mul=-1.0 / EMB)
 
-            centred = stage2.tile([P, PACK, EMB], F32)
-            for j in range(PACK):
+            if s + LEAD < PAIRS:
+                transpose(s + LEAD)
+
+            if waiting is not None:
+                finish(*waiting[:3], rstd_before)
+
+            centred = stage2.tile([P, PAIR, EMB], F32)
+            for i in range(PAIR):
+                if on_vector(s, i):
+                    nc.vector.bn_aggr(out=moments[:], in_=stats[:])
+            for i in sorted(range(PAIR), key=lambda i: on_vector(s, i)):
                 nc.vector.scalar_tensor_tensor(
-                    out=centred[:, j, :],
-                    in0=h[:, j, :],
-                    scalar=neg_mean[:, j : j + 1],
+                    out=centred[:, i, :],
+                    in0=h_banks[i][:] if on_vector(s, i) else h[:, i, :],
+                    scalar=moments[:, 0:1] if on_vector(s, i) else mean[:, i : i + 1],
                     in1=gamma_all[:],
-                    op0=ALU.add,
+                    op0=ALU.subtract if on_vector(s, i) else ALU.add,
                     op1=ALU.mult,
                 )
 
-            if g + LEAD < GROUPS:
-                transpose_and_quantise(g + LEAD)
+            if s + LEAD < PAIRS:
+                quantise_turned(s + LEAD)
 
-            square_sum = stage2.tile([P, PACK], F32)
-            for j in range(PACK):
-                squares = stage2.tile([P, EMB], BF16)
-                nc.scalar.activation(
-                    out=squares[:],
-                    in_=h[:, j, :],
-                    func=ACT.Square,
-                    bias=neg_mean[:, j : j + 1],
-                    accum_out=square_sum[:, j : j + 1],
-                )
-            std = stage2.tile([P, PACK], F32)
-            nc.scalar.activation(out=std[:], in_=square_sum[:], func=ACT.Sqrt, bias=LN_EPS, scale=1.0 / EMB)
-            rstd = stage2.tile([P, PACK], F32)
-            nc.vector.reciprocal(out=rstd[:], in_=std[:])
+            square_sum = stage2.tile([P, PAIR], F32)
+            std = stage2.tile([P, PAIR], F32)
+            for i in range(PAIR):
+                if not on_vector(s, i):
+                    squares = stage2.tile([P, EMB], BF16)
+                    nc.scalar.activation(
+                        out=squares[:],
+                        in_=h[:, i, :],
+                        func=ACT.Square,
+                        bias=mean[:, i : i + 1],
+                        accum_out=square_sum[:, i : i + 1],
+                    )
+            nc.scalar.activation(
+                out=std[:, on_scalar], in_=square_sum[:, on_scalar], func=ACT.Sqrt, bias=LN_EPS, scale=1.0 / EMB
+            )
+            if on_vector(s, 1):
+                nc.scalar.activation(out=std[:, 1:2], in_=moments[:, 1:2], func=ACT.Sqrt, bias=LN_EPS)
 
-            result = result_tiles[g]
-            for j in range(PACK):
-                nc.vector.scalar_tensor_tensor(
-                    out=result[:, j, :],
-                    in0=centred[:, j, :],
-                    scalar=rstd[:, j : j + 1],
-                    in1=result[:, j, :],
-                    op0=ALU.mult,
-                    op1=ALU.add,
-                )
-                nc.sync.dma_start(out=node_rows(out, g)[:, j * EMB : (j + 1) * EMB], in_=result[:, j, :])
+            waiting = (s, residual(s), centred, std)
+        finish(*waiting[:3], invert(waiting[3]))

@@ -161,16 +161,13 @@ def tile_hgnnmodel_pa_t_kernel(tc, e_nodes, adj, ego_embeddings, ln_gamma, ln_be
                 ego_rows.append(ego_tile)
 
         stage2 = ctx.enter_context(tc.tile_pool(name="stage2", bufs=3))
-        codes_pool = ctx.enter_context(tc.tile_pool(name="stage2_codes", bufs=LEAD + 1))
+        codes_pool = ctx.enter_context(tc.tile_pool(name="stage2_codes", bufs=LEAD + 2))
+        turned_banks = []
         turned_words = []
         adjT_codes = []
         adjT_scales = []
 
         def transpose(s):
-            grouped = stage2.tile([P, EDGE_PASSES * PAIR * P * PACK], BF16, align_bytes=64, name="adjT_grouped")
-            grouped_words = grouped[:].bitcast(F32).rearrange(
-                "p (k j r u) -> p k j r u", k=EDGE_PASSES, j=PAIR, r=P, u=2
-            )
             row_words = EDGES // 2
             words = adj_rows[s * PAIR // PACK][:].bitcast(F32)
             for i in range(PAIR):
@@ -182,11 +179,17 @@ def tile_hgnnmodel_pa_t_kernel(tc, e_nodes, adj, ego_embeddings, ln_gamma, ln_be
                         words[:, j * row_words + c * P : j * row_words + (c + 1) * P],
                         identity[:],
                     )
-                nc.scalar.copy(
-                    out=grouped_words[:, :, i],
-                    in_=turned[:].rearrange("p (k u r) -> p k r u", k=EDGE_PASSES, u=2),
-                )
+                turned_banks.append(turned)
+            grouped = stage2.tile([P, EDGE_PASSES * PAIR * P * PACK], BF16, align_bytes=64, name="adjT_grouped")
             turned_words.append(grouped)
+
+        def empty_turned(s, i):
+            nc.scalar.copy(
+                out=turned_words[s][:].bitcast(F32).rearrange(
+                    "p (k j r u) -> p k j r u", k=EDGE_PASSES, j=PAIR, r=P, u=2
+                )[:, :, i],
+                in_=turned_banks[s * PAIR + i][:].rearrange("p (k u r) -> p k r u", k=EDGE_PASSES, u=2),
+            )
 
         def quantise_turned(s):
             codes = codes_pool.tile([P, EDGE_PASSES * PAIR * P], U32, align_bytes=64, name="adjT_codes")
@@ -223,12 +226,13 @@ def tile_hgnnmodel_pa_t_kernel(tc, e_nodes, adj, ego_embeddings, ln_gamma, ln_be
             empty_m_bank(t)
         quantise_m(0)
         regroup_m(1)
-        transpose(0)
-        quantise_turned(0)
-        quantise_m(1)
-        for s in range(1, LEAD):
+        for s in range(LEAD):
             transpose(s)
+            for i in range(PAIR):
+                empty_turned(s, i)
             quantise_turned(s)
+            if s == 0:
+                quantise_m(1)
 
         VECTOR_RESIDUAL = PACK - 1
 
@@ -255,11 +259,6 @@ def tile_hgnnmodel_pa_t_kernel(tc, e_nodes, adj, ego_embeddings, ln_gamma, ln_be
         def on_vector(s, i):
             return (s * PAIR + i) % 8 == 1
 
-        def invert(std):
-            rstd = stage2.tile([P, PAIR], F32)
-            nc.vector.reciprocal(out=rstd[:], in_=std[:])
-            return rstd
-
         def finish(s, residuals, centred, rstd):
             for i in range(PAIR):
                 g, j = divmod(s * PAIR + i, PACK)
@@ -274,82 +273,104 @@ def tile_hgnnmodel_pa_t_kernel(tc, e_nodes, adj, ego_embeddings, ln_gamma, ln_be
                 )
                 nc.sync.dma_start(out=node_rows(out, g)[:, j * EMB : (j + 1) * EMB], in_=result[:])
 
-        waiting = None
-        for s in range(PAIRS):
-            h_banks = []
-            for i in range(PAIR):
-                h_bank = bank("sums")
-                for k in range(EDGE_PASSES):
-                    cols = slice((k * PAIR + i) * P, (k * PAIR + i + 1) * P)
-                    nc.tensor.matmul_mx(
-                        out=h_bank[:],
-                        lhsT=adjT_codes[s][:, cols].bitcast(FP8X4),
-                        lhsT_scale=adjT_scales[s][:, cols],
-                        rhs=m_codes[:, k, :].bitcast(FP8X4),
-                        rhs_scale=m_scales[:, k, :],
-                        start=(k == 0),
-                        stop=(k == EDGE_PASSES - 1),
-                    )
-                h_banks.append(h_bank)
+        centred_of = []
+        square_sums = []
+        moments_of = []
+        for s in range(PAIRS + 1):
+            current = s < PAIRS
+            before = s > 0
+            ahead = s + LEAD < PAIRS
+            on_scalar = slice(0, 1) if on_vector(s, 1) else slice(0, PAIR)
+            on_scalar_before = slice(0, 1) if on_vector(s - 1, 1) else slice(0, PAIR)
 
-            if waiting is not None:
-                rstd_before = invert(waiting[3])
+            h_banks = []
+            if current:
+                for i in range(PAIR):
+                    h_bank = bank("sums")
+                    for k in range(EDGE_PASSES):
+                        cols = slice((k * PAIR + i) * P, (k * PAIR + i + 1) * P)
+                        nc.tensor.matmul_mx(
+                            out=h_bank[:],
+                            lhsT=adjT_codes[s][:, cols].bitcast(FP8X4),
+                            lhsT_scale=adjT_scales[s][:, cols],
+                            rhs=m_codes[:, k, :].bitcast(FP8X4),
+                            rhs_scale=m_scales[:, k, :],
+                            start=(k == 0),
+                            stop=(k == EDGE_PASSES - 1),
+                        )
+                    h_banks.append(h_bank)
+            if before:
+                residuals = residual(s - 1)
+            if ahead:
+                transpose(s + LEAD)
 
             h = stage2.tile([P, PAIR, EMB], F32)
             row_sum = stage2.tile([P, PAIR], F32)
-            mean = stage2.tile([P, PAIR], F32)
+            neg_mean = stage2.tile([P, PAIR], F32)
             stats = stage2.tile([P, 6], F32)
             moments = stage2.tile([P, 2], F32)
-            for i in range(PAIR):
-                if on_vector(s, i):
-                    nc.vector.bn_stats(out=stats[:], in_=h_banks[i][:])
-                else:
+            if current:
+                for i in range(PAIR):
+                    if on_vector(s, i):
+                        nc.vector.bn_stats(out=stats[:], in_=h_banks[i][:])
+                    else:
+                        nc.scalar.activation(
+                            out=h[:, i, :], in_=h_banks[i][:], func=ACT.Identity, accum_out=row_sum[:, i : i + 1]
+                        )
+            if ahead:
+                empty_turned(s + LEAD, 0)
+            if current:
+                nc.scalar.mul(out=neg_mean[:, on_scalar], in_=row_sum[:, on_scalar], mul=-1.0 / EMB)
+            if ahead:
+                empty_turned(s + LEAD, 1)
+            if before:
+                std = stage2.tile([P, PAIR], F32)
+                nc.scalar.activation(
+                    out=std[:, on_scalar_before],
+                    in_=square_sums[s - 1][:, on_scalar_before],
+                    func=ACT.Sqrt,
+                    bias=LN_EPS,
+                    scale=1.0 / EMB,
+                )
+                if on_vector(s - 1, 1):
                     nc.scalar.activation(
-                        out=h[:, i, :], in_=h_banks[i][:], func=ACT.Identity, accum_out=row_sum[:, i : i + 1]
+                        out=std[:, 1:2], in_=moments_of[s - 1][:, 1:2], func=ACT.Sqrt, bias=LN_EPS
                     )
-            on_scalar = slice(0, 1) if on_vector(s, 1) else slice(0, PAIR)
-            nc.scalar.mul(out=mean[:, on_scalar], in_=row_sum[:, on_scalar], mul=-1.0 / EMB)
-
-            if s + LEAD < PAIRS:
-                transpose(s + LEAD)
-
-            if waiting is not None:
-                finish(*waiting[:3], rstd_before)
 
             centred = stage2.tile([P, PAIR, EMB], F32)
+            rstd = stage2.tile([P, PAIR], F32)
             for i in range(PAIR):
-                if on_vector(s, i):
+                if current:
+                    vector = on_vector(s, i)
+                    nc.vector.scalar_tensor_tensor(
+                        out=centred[:, i, :],
+                        in0=h_banks[i][:] if vector else h[:, i, :],
+                        scalar=moments[:, 0:1] if vector else neg_mean[:, i : i + 1],
+                        in1=gamma_all[:],
+                        op0=ALU.subtract if vector else ALU.add,
+                        op1=ALU.mult,
+                    )
+                if i == 0 and current and on_vector(s, 1):
                     nc.vector.bn_aggr(out=moments[:], in_=stats[:])
-            for i in sorted(range(PAIR), key=lambda i: on_vector(s, i)):
-                nc.vector.scalar_tensor_tensor(
-                    out=centred[:, i, :],
-                    in0=h_banks[i][:] if on_vector(s, i) else h[:, i, :],
-                    scalar=moments[:, 0:1] if on_vector(s, i) else mean[:, i : i + 1],
-                    in1=gamma_all[:],
-                    op0=ALU.subtract if on_vector(s, i) else ALU.add,
-                    op1=ALU.mult,
-                )
-
-            if s + LEAD < PAIRS:
+                if i == 0 and before:
+                    nc.vector.reciprocal(out=rstd[:], in_=std[:])
+            if ahead:
                 quantise_turned(s + LEAD)
+            if before:
+                finish(s - 1, residuals, centred_of[s - 1], rstd)
 
             square_sum = stage2.tile([P, PAIR], F32)
-            std = stage2.tile([P, PAIR], F32)
-            for i in range(PAIR):
-                if not on_vector(s, i):
-                    squares = stage2.tile([P, EMB], BF16)
-                    nc.scalar.activation(
-                        out=squares[:],
-                        in_=h[:, i, :],
-                        func=ACT.Square,
-                        bias=mean[:, i : i + 1],
-                        accum_out=square_sum[:, i : i + 1],
-                    )
-            nc.scalar.activation(
-                out=std[:, on_scalar], in_=square_sum[:, on_scalar], func=ACT.Sqrt, bias=LN_EPS, scale=1.0 / EMB
-            )
-            if on_vector(s, 1):
-                nc.scalar.activation(out=std[:, 1:2], in_=moments[:, 1:2], func=ACT.Sqrt, bias=LN_EPS)
-
-            waiting = (s, residual(s), centred, std)
-        finish(*waiting[:3], invert(waiting[3]))
+            if current:
+                for i in range(PAIR):
+                    if not on_vector(s, i):
+                        squares = stage2.tile([P, EMB], BF16)
+                        nc.scalar.activation(
+                            out=squares[:],
+                            in_=h[:, i, :],
+                            func=ACT.Square,
+                            bias=neg_mean[:, i : i + 1],
+                            accum_out=square_sum[:, i : i + 1],
+                        )
+            centred_of.append(centred)
+            square_sums.append(square_sum)
+            moments_of.append(moments)

@@ -20,6 +20,7 @@ EDGE_PASSES = EDGES // K_PASS
 EDGE_TILES = EDGES // P
 QUARTERS = EDGES // (2 * P)
 LN_EPS = 1e-5
+VECTOR_RUNS = 12
 LOAD_AHEAD = 3
 PAIR = 2
 PAIRS = NODES // (PAIR * P)
@@ -53,12 +54,16 @@ def tile_hgnnmodel_pa_t_kernel(tc, e_nodes, adj, ego_embeddings, ln_gamma, ln_be
         ones = consts.tile([P, P], BF16)
         nc.vector.memset(ones[:], 1.0)
         table_warmer = consts.tile([P, 1], F32)
-        nc.scalar.sqrt(out=table_warmer[:], in_=ones[:, 0:1])
+        nc.scalar.activation(out=table_warmer[:], in_=ones[:, 0:1], func=ACT.Abs_reciprocal_sqrt)
         vector_rows = consts.tile([P, 2 * EMB], BF16)
         nc.vector.memset(vector_rows[:], 0.0)
         nc.scalar.dma_start(out=vector_rows[0:1, 0:EMB], in_=ln_gamma.unsqueeze(0))
         nc.scalar.dma_start(out=vector_rows[0:1, EMB : 2 * EMB], in_=ln_beta.unsqueeze(0))
         adj_rows = []
+
+        def adj_pieces(g):
+            return 2 if g == 0 else 1
+
         e_rows = []
         adj_grouped = []
         e_grouped = []
@@ -73,40 +78,36 @@ def tile_hgnnmodel_pa_t_kernel(tc, e_nodes, adj, ego_embeddings, ln_gamma, ln_be
                 nc.sync.dma_start(out=e_tile[:], in_=node_rows(e_nodes, g))
                 e_rows.append(e_tile)
                 adj_tile = resident.tile([P, PACK * EDGES], BF16, name="adj_rows%d" % g)
-                pieces = 2 if g == 0 else 1
-                for h in range(pieces):
-                    cols = slice(h * EDGES // pieces, (h + 1) * EDGES // pieces)
+                pieces = adj_pieces(g)
+                for b in range(pieces):
                     nc.sync.dma_start(
-                        out=adj_tile[:].rearrange("p (j c) -> p j c", j=PACK)[:, :, cols],
-                        in_=node_rows(adj, g).rearrange("p (j c) -> p j c", j=PACK)[:, :, cols],
+                        out=adj_tile[:].rearrange("p (b j c) -> p b j c", b=pieces, j=PACK)[:, b],
+                        in_=node_rows(adj, g).rearrange("p (j b c) -> p b j c", b=pieces, j=PACK)[:, b],
                     )
                 adj_rows.append(adj_tile)
 
             def regroup(g):
                 adj_tile = stage1.tile([P, EDGES, PACK], BF16, align_bytes=64, name="adj_grouped")
-                dst = adj_tile[:].rearrange("p (a s c i) j -> p s a c j i", a=QUARTERS, s=2, i=4)
-                src = adj_rows[g][:].rearrange("p (j a c i s) -> p s a c j i", j=PACK, a=QUARTERS, i=4, s=2)
+                pieces = adj_pieces(g)
+                dst = adj_tile[:].rearrange("p (b a s c i) j -> p b s a c j i", b=pieces, a=QUARTERS // pieces, s=2, i=4)
+                src = adj_rows[g][:].rearrange(
+                    "p (b j a c i s) -> p b s a c j i", b=pieces, j=PACK, a=QUARTERS // pieces, i=4, s=2
+                )
                 e_tile = stage1.tile([P, EMB, PACK], BF16, align_bytes=64, name="e_grouped")
                 nc.scalar.copy(
                     out=e_tile[:].rearrange("p (c i) j -> p c j i", i=4),
                     in_=e_rows[g][:].rearrange("p (j c i) -> p c j i", j=PACK, i=4),
                 )
-                for s in range(2):
-                    nc.vector.tensor_copy(out=dst[:, s, 0 : QUARTERS // 2], in_=src[:, s, 0 : QUARTERS // 2])
-                nc.vector.tensor_copy(out=dst[:, 0, QUARTERS // 2 :], in_=src[:, 0, QUARTERS // 2 :])
-                for a in range(QUARTERS // 2, QUARTERS):
-                    nc.scalar.copy(out=dst[:, 1, a], in_=src[:, 1, a])
+                for b in range(pieces):
+                    nc.vector.tensor_copy(out=dst[:, b, 0], in_=src[:, b, 0])
+                    nc.vector.tensor_copy(out=dst[:, b, 1, :, :VECTOR_RUNS], in_=src[:, b, 1, :, :VECTOR_RUNS])
+                    nc.scalar.copy(out=dst[:, b, 1, :, VECTOR_RUNS:], in_=src[:, b, 1, :, VECTOR_RUNS:])
                 adj_grouped.append(adj_tile)
                 e_grouped.append(e_tile)
 
-            def quantise_and_multiply(g):
-                adj_codes = stage1_codes.tile([P, EDGES], U32, align_bytes=64)
-                adj_scales = stage1_codes.tile([P, EDGES], U8, align_bytes=64)
-                nc.vector.quantize_mx(
-                    out=adj_codes[:].bitcast(FP8X4),
-                    scales=adj_scales[:],
-                    in_=adj_grouped[g][:].rearrange("p w j -> p (w j)"),
-                )
+            codes_of = []
+
+            def quantise(g):
                 e_codes = stage1_codes.tile([P, EMB], U32, align_bytes=64)
                 e_scales = stage1_codes.tile([P, EMB], U8, align_bytes=64)
                 nc.vector.quantize_mx(
@@ -114,6 +115,17 @@ def tile_hgnnmodel_pa_t_kernel(tc, e_nodes, adj, ego_embeddings, ln_gamma, ln_be
                     scales=e_scales[:],
                     in_=e_grouped[g][:].rearrange("p w j -> p (w j)"),
                 )
+                adj_codes = stage1_codes.tile([P, EDGES], U32, align_bytes=64)
+                adj_scales = stage1_codes.tile([P, EDGES], U8, align_bytes=64)
+                nc.vector.quantize_mx(
+                    out=adj_codes[:].bitcast(FP8X4),
+                    scales=adj_scales[:],
+                    in_=adj_grouped[g][:].rearrange("p w j -> p (w j)"),
+                )
+                codes_of.append((adj_codes, adj_scales, e_codes, e_scales))
+
+            def multiply(g):
+                adj_codes, adj_scales, e_codes, e_scales = codes_of[g]
                 for t in range(EDGE_TILES):
                     nc.tensor.matmul_mx(
                         out=m_banks[t][:],
@@ -129,6 +141,7 @@ def tile_hgnnmodel_pa_t_kernel(tc, e_nodes, adj, ego_embeddings, ln_gamma, ln_be
                 load_group(g)
             for g in range(2):
                 regroup(g)
+                quantise(g)
             gamma_all = consts.tile([P, EMB], F32)
             beta_all = consts.tile([P, EMB], F32)
             for i, spread in enumerate((gamma_all, beta_all)):
@@ -148,9 +161,8 @@ def tile_hgnnmodel_pa_t_kernel(tc, e_nodes, adj, ego_embeddings, ln_gamma, ln_be
                     load_group(g + LOAD_AHEAD)
                 if g > 1:
                     regroup(g)
-                if g > 0:
-                    quantise_and_multiply(g - 1)
-            quantise_and_multiply(GROUPS - 1)
+                    quantise(g)
+                multiply(g)
 
             ego_rows = []
             for g in range(GROUPS):
@@ -168,17 +180,17 @@ def tile_hgnnmodel_pa_t_kernel(tc, e_nodes, adj, ego_embeddings, ln_gamma, ln_be
         adjT_scales = []
 
         def transpose(s):
-            row_words = EDGES // 2
-            words = adj_rows[s * PAIR // PACK][:].bitcast(F32)
+            g = s * PAIR // PACK
+            pieces = adj_pieces(g)
+            words = adj_rows[g][:].bitcast(F32).rearrange(
+                "p (b j c q) -> p b c j q", b=pieces, j=PACK, q=P
+            )
             for i in range(PAIR):
                 j = (s * PAIR + i) % PACK
                 turned = bank("turned")
                 for c in range(2 * EDGE_PASSES):
-                    nc.tensor.transpose(
-                        turned[:, c * P : (c + 1) * P],
-                        words[:, j * row_words + c * P : j * row_words + (c + 1) * P],
-                        identity[:],
-                    )
+                    b, rest = divmod(c, 2 * EDGE_PASSES // pieces)
+                    nc.tensor.transpose(turned[:, c * P : (c + 1) * P], words[:, b, rest, j], identity[:])
                 turned_banks.append(turned)
             grouped = stage2.tile([P, EDGE_PASSES * PAIR * P * PACK], BF16, align_bytes=64, name="adjT_grouped")
             turned_words.append(grouped)
@@ -197,6 +209,16 @@ def tile_hgnnmodel_pa_t_kernel(tc, e_nodes, adj, ego_embeddings, ln_gamma, ln_be
             nc.vector.quantize_mx(out=codes[:].bitcast(FP8X4), scales=scales[:], in_=turned_words[s][:])
             adjT_codes.append(codes)
             adjT_scales.append(scales)
+
+        VECTOR_RESIDUAL = PACK - 1
+        vector_residuals = []
+
+        def vector_residual(g):
+            tile = resident.tile([P, EMB], F32, name="vector_residual%d" % g)
+            nc.vector.tensor_tensor(
+                out=tile[:], in0=ego_rows[g][:, VECTOR_RESIDUAL, :], in1=beta_all[:], op=ALU.add
+            )
+            vector_residuals.append(tile)
 
         m_grouped = resident.tile([P, EDGE_PASSES, EMB, PACK], BF16, align_bytes=64)
         m_codes = resident.tile([P, EDGE_PASSES, EMB], U32, align_bytes=64)
@@ -219,6 +241,8 @@ def tile_hgnnmodel_pa_t_kernel(tc, e_nodes, adj, ego_embeddings, ln_gamma, ln_be
                 in_=m_grouped[:, k].rearrange("p f t -> p (f t)"),
             )
 
+        for g in range(GROUPS // 2):
+            vector_residual(g)
         for t in range(PACK):
             empty_m_bank(t)
         regroup_m(0)
@@ -233,18 +257,15 @@ def tile_hgnnmodel_pa_t_kernel(tc, e_nodes, adj, ego_embeddings, ln_gamma, ln_be
             quantise_turned(s)
             if s == 0:
                 quantise_m(1)
-
-        VECTOR_RESIDUAL = PACK - 1
+        for g in range(GROUPS // 2, GROUPS):
+            vector_residual(g)
 
         def residual(s):
             tiles = []
             for i in range(PAIR):
                 g, j = divmod(s * PAIR + i, PACK)
                 if j == VECTOR_RESIDUAL:
-                    tile = stage2.tile([P, EMB], F32, name="vector_residual")
-                    nc.vector.tensor_tensor(
-                        out=tile[:], in0=ego_rows[g][:, j, :], in1=beta_all[:], op=ALU.add
-                    )
+                    tile = vector_residuals[g]
                 else:
                     tile = bank("residual")
                     nc.tensor.matmul(
@@ -257,7 +278,7 @@ def tile_hgnnmodel_pa_t_kernel(tc, e_nodes, adj, ego_embeddings, ln_gamma, ln_be
             return tiles
 
         def on_vector(s, i):
-            return (s * PAIR + i) % 8 == 1
+            return i == 1 and s % 5 == 0
 
         def finish(s, residuals, centred, rstd):
             for i in range(PAIR):
@@ -324,21 +345,23 @@ def tile_hgnnmodel_pa_t_kernel(tc, e_nodes, adj, ego_embeddings, ln_gamma, ln_be
             if ahead:
                 empty_turned(s + LEAD, 1)
             if before:
-                std = stage2.tile([P, PAIR], F32)
+                rstd = stage2.tile([P, PAIR], F32)
                 nc.scalar.activation(
-                    out=std[:, on_scalar_before],
+                    out=rstd[:, on_scalar_before],
                     in_=square_sums[s - 1][:, on_scalar_before],
-                    func=ACT.Sqrt,
+                    func=ACT.Abs_reciprocal_sqrt,
                     bias=LN_EPS,
                     scale=1.0 / EMB,
                 )
                 if on_vector(s - 1, 1):
                     nc.scalar.activation(
-                        out=std[:, 1:2], in_=moments_of[s - 1][:, 1:2], func=ACT.Sqrt, bias=LN_EPS
+                        out=rstd[:, 1:2],
+                        in_=moments_of[s - 1][:, 1:2],
+                        func=ACT.Abs_reciprocal_sqrt,
+                        bias=LN_EPS,
                     )
 
             centred = stage2.tile([P, PAIR, EMB], F32)
-            rstd = stage2.tile([P, PAIR], F32)
             for i in range(PAIR):
                 if current:
                     vector = on_vector(s, i)
@@ -352,8 +375,6 @@ def tile_hgnnmodel_pa_t_kernel(tc, e_nodes, adj, ego_embeddings, ln_gamma, ln_be
                     )
                 if i == 0 and current and on_vector(s, 1):
                     nc.vector.bn_aggr(out=moments[:], in_=stats[:])
-                if i == 0 and before:
-                    nc.vector.reciprocal(out=rstd[:], in_=std[:])
             if ahead:
                 quantise_turned(s + LEAD)
             if before:

@@ -20,7 +20,7 @@ EDGE_PASSES = EDGES // K_PASS
 EDGE_TILES = EDGES // P
 QUARTERS = EDGES // (2 * P)
 LN_EPS = 1e-5
-VECTOR_RUNS = 12
+VECTOR_RUNS = 16
 LOAD_AHEAD = 3
 PAIR = 2
 PAIRS = NODES // (PAIR * P)

@@ -55,10 +55,11 @@ def tile_hgnnmodel_pa_t_kernel(tc, e_nodes, adj, ego_embeddings, ln_gamma, ln_be
         nc.vector.memset(ones[:], 1.0)
         table_warmer = consts.tile([P, 1], F32)
         nc.scalar.activation(out=table_warmer[:], in_=ones[:, 0:1], func=ACT.Abs_reciprocal_sqrt)
-        vector_rows = consts.tile([P, 2 * EMB], BF16)
-        nc.vector.memset(vector_rows[:], 0.0)
-        nc.scalar.dma_start(out=vector_rows[0:1, 0:EMB], in_=ln_gamma.unsqueeze(0))
-        nc.scalar.dma_start(out=vector_rows[0:1, EMB : 2 * EMB], in_=ln_beta.unsqueeze(0))
+        beta_row = consts.tile([P, EMB], BF16)
+        nc.vector.memset(beta_row[:], 0.0)
+        nc.scalar.dma_start(out=beta_row[0:1, :], in_=ln_beta.unsqueeze(0))
+        gamma_all = consts.tile([P, EMB], BF16)
+
         adj_rows = []
 
         def adj_pieces(g):
@@ -139,29 +140,13 @@ def tile_hgnnmodel_pa_t_kernel(tc, e_nodes, adj, ego_embeddings, ln_gamma, ln_be
 
             for g in range(LOAD_AHEAD):
                 load_group(g)
-            for g in range(2):
-                regroup(g)
-                quantise(g)
-            gamma_all = consts.tile([P, EMB], F32)
-            beta_all = consts.tile([P, EMB], F32)
-            for i, spread in enumerate((gamma_all, beta_all)):
-                spread_bank = bank("sums")
-                nc.tensor.matmul(
-                    out=spread_bank[:],
-                    lhsT=ones[:],
-                    rhs=vector_rows[:, i * EMB : (i + 1) * EMB],
-                    start=True,
-                    stop=True,
-                )
-                nc.scalar.copy(out=spread[:], in_=spread_bank[:])
             m_tags = ("turned", "turned", "sums", "sums", "sums", "residual", "residual", "residual")
             m_banks = [bank(m_tags[t], name="m_bank%d" % t) for t in range(EDGE_TILES)]
             for g in range(GROUPS):
                 if g + LOAD_AHEAD < GROUPS:
                     load_group(g + LOAD_AHEAD)
-                if g > 1:
-                    regroup(g)
-                    quantise(g)
+                regroup(g)
+                quantise(g)
                 multiply(g)
 
             ego_rows = []
@@ -171,6 +156,8 @@ def tile_hgnnmodel_pa_t_kernel(tc, e_nodes, adj, ego_embeddings, ln_gamma, ln_be
                     out=ego_tile[:].rearrange("p j f -> p (j f)"), in_=node_rows(ego_embeddings, g)
                 )
                 ego_rows.append(ego_tile)
+                if g == 1:
+                    nc.sync.dma_start(out=gamma_all[:], in_=ln_gamma.partition_broadcast(P))
 
         stage2 = ctx.enter_context(tc.tile_pool(name="stage2", bufs=3))
         codes_pool = ctx.enter_context(tc.tile_pool(name="stage2_codes", bufs=LEAD + 2))
@@ -192,7 +179,7 @@ def tile_hgnnmodel_pa_t_kernel(tc, e_nodes, adj, ego_embeddings, ln_gamma, ln_be
                     b, rest = divmod(c, 2 * EDGE_PASSES // pieces)
                     nc.tensor.transpose(turned[:, c * P : (c + 1) * P], words[:, b, rest, j], identity[:])
                 turned_banks.append(turned)
-            grouped = stage2.tile([P, EDGE_PASSES * PAIR * P * PACK], BF16, align_bytes=64, name="adjT_grouped")
+            grouped = stage2.tile([P, EDGE_PASSES * PAIR * P * PACK], BF16, align_bytes=64, name="adjT_grouped", bufs=LEAD)
             turned_words.append(grouped)
 
         def empty_turned(s, i):
@@ -209,16 +196,6 @@ def tile_hgnnmodel_pa_t_kernel(tc, e_nodes, adj, ego_embeddings, ln_gamma, ln_be
             nc.vector.quantize_mx(out=codes[:].bitcast(FP8X4), scales=scales[:], in_=turned_words[s][:])
             adjT_codes.append(codes)
             adjT_scales.append(scales)
-
-        VECTOR_RESIDUAL = PACK - 1
-        vector_residuals = []
-
-        def vector_residual(g):
-            tile = resident.tile([P, EMB], F32, name="vector_residual%d" % g)
-            nc.vector.tensor_tensor(
-                out=tile[:], in0=ego_rows[g][:, VECTOR_RESIDUAL, :], in1=beta_all[:], op=ALU.add
-            )
-            vector_residuals.append(tile)
 
         m_grouped = resident.tile([P, EDGE_PASSES, EMB, PACK], BF16, align_bytes=64)
         m_codes = resident.tile([P, EDGE_PASSES, EMB], U32, align_bytes=64)
@@ -241,8 +218,6 @@ def tile_hgnnmodel_pa_t_kernel(tc, e_nodes, adj, ego_embeddings, ln_gamma, ln_be
                 in_=m_grouped[:, k].rearrange("p f t -> p (f t)"),
             )
 
-        for g in range(GROUPS // 2):
-            vector_residual(g)
         for t in range(PACK):
             empty_m_bank(t)
         regroup_m(0)
@@ -257,28 +232,40 @@ def tile_hgnnmodel_pa_t_kernel(tc, e_nodes, adj, ego_embeddings, ln_gamma, ln_be
             quantise_turned(s)
             if s == 0:
                 quantise_m(1)
-        for g in range(GROUPS // 2, GROUPS):
-            vector_residual(g)
+        turned_beta = consts.tile([P, EMB], F32)
+        beta_bank = bank("residual")
+        for c in range(EMB // P):
+            cols = slice(c * P, (c + 1) * P)
+            nc.tensor.matmul(
+                out=beta_bank[:, cols], lhsT=beta_row[:, cols], rhs=ones[:], start=True, stop=True
+            )
+        nc.scalar.copy(out=turned_beta[:], in_=beta_bank[:])
 
         def residual(s):
             tiles = []
             for i in range(PAIR):
                 g, j = divmod(s * PAIR + i, PACK)
-                if j == VECTOR_RESIDUAL:
-                    tile = vector_residuals[g]
-                else:
-                    tile = bank("residual")
-                    nc.tensor.matmul(
-                        out=tile[:], lhsT=identity_bf16[:], rhs=ego_rows[g][:, j, :], start=True, stop=False
-                    )
-                    nc.tensor.matmul(
-                        out=tile[:], lhsT=ones[:], rhs=vector_rows[:, EMB : 2 * EMB], start=False, stop=True
-                    )
-                tiles.append(tile)
+                added = bank("residual")
+                nc.tensor.matmul(
+                    out=added[:], lhsT=identity_bf16[:], rhs=ego_rows[g][:, j, :], start=True, stop=False
+                )
+                if i == 0:
+                    nc.tensor.matmul(out=added[:], lhsT=ones[:], rhs=beta_row[:], start=False, stop=True)
+                tiles.append(added)
+            for c in range(EMB // P):
+                cols = slice(c * P, (c + 1) * P)
+                nc.tensor.matmul(
+                    out=tiles[1][:, cols],
+                    lhsT=turned_beta[:, cols],
+                    rhs=identity[:],
+                    start=False,
+                    stop=(c == EMB // P - 1),
+                    is_transpose=True,
+                )
             return tiles
 
         def on_vector(s, i):
-            return i == 1 and s % 5 == 0
+            return i == 1 and s % 5 in (0, 2)
 
         def finish(s, residuals, centred, rstd):
             for i in range(PAIR):
@@ -294,6 +281,25 @@ def tile_hgnnmodel_pa_t_kernel(tc, e_nodes, adj, ego_embeddings, ln_gamma, ln_be
                 )
                 nc.sync.dma_start(out=node_rows(out, g)[:, j * EMB : (j + 1) * EMB], in_=result[:])
 
+        def multiply_turned(s):
+            h_banks = []
+            for i in range(PAIR):
+                h_bank = bank("sums")
+                for k in range(EDGE_PASSES):
+                    cols = slice((k * PAIR + i) * P, (k * PAIR + i + 1) * P)
+                    nc.tensor.matmul_mx(
+                        out=h_bank[:],
+                        lhsT=adjT_codes[s][:, cols].bitcast(FP8X4),
+                        lhsT_scale=adjT_scales[s][:, cols],
+                        rhs=m_codes[:, k, :].bitcast(FP8X4),
+                        rhs_scale=m_scales[:, k, :],
+                        start=(k == 0),
+                        stop=(k == EDGE_PASSES - 1),
+                    )
+                h_banks.append(h_bank)
+            return h_banks
+
+        next_banks = multiply_turned(0)
         centred_of = []
         square_sums = []
         moments_of = []
@@ -304,26 +310,13 @@ def tile_hgnnmodel_pa_t_kernel(tc, e_nodes, adj, ego_embeddings, ln_gamma, ln_be
             on_scalar = slice(0, 1) if on_vector(s, 1) else slice(0, PAIR)
             on_scalar_before = slice(0, 1) if on_vector(s - 1, 1) else slice(0, PAIR)
 
-            h_banks = []
-            if current:
-                for i in range(PAIR):
-                    h_bank = bank("sums")
-                    for k in range(EDGE_PASSES):
-                        cols = slice((k * PAIR + i) * P, (k * PAIR + i + 1) * P)
-                        nc.tensor.matmul_mx(
-                            out=h_bank[:],
-                            lhsT=adjT_codes[s][:, cols].bitcast(FP8X4),
-                            lhsT_scale=adjT_scales[s][:, cols],
-                            rhs=m_codes[:, k, :].bitcast(FP8X4),
-                            rhs_scale=m_scales[:, k, :],
-                            start=(k == 0),
-                            stop=(k == EDGE_PASSES - 1),
-                        )
-                    h_banks.append(h_bank)
-            if before:
-                residuals = residual(s - 1)
             if ahead:
                 transpose(s + LEAD)
+            h_banks = next_banks
+            if s + 1 < PAIRS:
+                next_banks = multiply_turned(s + 1)
+            if before:
+                residuals = residual(s - 1)
 
             h = stage2.tile([P, PAIR, EMB], F32)
             row_sum = stage2.tile([P, PAIR], F32)

@@ -24,7 +24,7 @@ VECTOR_RUNS = 16
 LOAD_AHEAD = 3
 PAIR = 2
 PAIRS = NODES // (PAIR * P)
-LEAD = 4
+LEAD = 3
 
 FLOPS = 2 * 2 * NODES * EDGES * EMB
 
@@ -118,11 +118,14 @@ def tile_hgnnmodel_pa_t_kernel(tc, e_nodes, adj, ego_embeddings, ln_gamma, ln_be
                 )
                 adj_codes = stage1_codes.tile([P, EDGES], U32, align_bytes=64)
                 adj_scales = stage1_codes.tile([P, EDGES], U8, align_bytes=64)
-                nc.vector.quantize_mx(
-                    out=adj_codes[:].bitcast(FP8X4),
-                    scales=adj_scales[:],
-                    in_=adj_grouped[g][:].rearrange("p w j -> p (w j)"),
-                )
+                pieces = 2 if g == GROUPS - 1 else 1
+                for b in range(pieces):
+                    cols = slice(b * EDGES // pieces, (b + 1) * EDGES // pieces)
+                    nc.vector.quantize_mx(
+                        out=adj_codes[:, cols].bitcast(FP8X4),
+                        scales=adj_scales[:, cols],
+                        in_=adj_grouped[g][:, cols].rearrange("p w j -> p (w j)"),
+                    )
                 codes_of.append((adj_codes, adj_scales, e_codes, e_scales))
 
             def multiply(g):
@@ -202,7 +205,7 @@ def tile_hgnnmodel_pa_t_kernel(tc, e_nodes, adj, ego_embeddings, ln_gamma, ln_be
         m_scales = resident.tile([P, EDGE_PASSES, EMB], U8, align_bytes=64)
 
         def empty_m_bank(t):
-            copy = nc.vector.tensor_copy if t % 2 else nc.scalar.copy
+            copy = nc.vector.tensor_copy if t in (0, 1, 7) else nc.scalar.copy
             copy(out=m_bf16[:, t, :], in_=m_banks[t][:])
 
         def regroup_m(k):
@@ -265,21 +268,20 @@ def tile_hgnnmodel_pa_t_kernel(tc, e_nodes, adj, ego_embeddings, ln_gamma, ln_be
             return tiles
 
         def on_vector(s, i):
-            return i == 1 and s % 5 in (0, 2)
+            return i == 1 and s % 3 == 0
 
-        def finish(s, residuals, centred, rstd):
-            for i in range(PAIR):
-                g, j = divmod(s * PAIR + i, PACK)
-                result = results.tile([P, EMB], F32)
-                nc.vector.scalar_tensor_tensor(
-                    out=result[:],
-                    in0=centred[:, i, :],
-                    scalar=rstd[:, i : i + 1],
-                    in1=residuals[i][:],
-                    op0=ALU.mult,
-                    op1=ALU.add,
-                )
-                nc.sync.dma_start(out=node_rows(out, g)[:, j * EMB : (j + 1) * EMB], in_=result[:])
+        def finish(s, i, residuals, centred, rstd):
+            g, j = divmod(s * PAIR + i, PACK)
+            result = results.tile([P, EMB], F32)
+            nc.vector.scalar_tensor_tensor(
+                out=result[:],
+                in0=centred[:, i, :],
+                scalar=rstd[:, i : i + 1],
+                in1=residuals[i][:],
+                op0=ALU.mult,
+                op1=ALU.add,
+            )
+            nc.sync.dma_start(out=node_rows(out, g)[:, j * EMB : (j + 1) * EMB], in_=result[:])
 
         def multiply_turned(s):
             h_banks = []
@@ -366,12 +368,16 @@ def tile_hgnnmodel_pa_t_kernel(tc, e_nodes, adj, ego_embeddings, ln_gamma, ln_be
                         op0=ALU.subtract if vector else ALU.add,
                         op1=ALU.mult,
                     )
-                if i == 0 and current and on_vector(s, 1):
-                    nc.vector.bn_aggr(out=moments[:], in_=stats[:])
-            if ahead:
-                quantise_turned(s + LEAD)
+                if i == 0:
+                    if current and on_vector(s, 1):
+                        nc.vector.bn_aggr(out=moments[:], in_=stats[:])
+                    if ahead:
+                        quantise_turned(s + LEAD)
+                    elif before:
+                        finish(s - 1, 0, residuals, centred_of[s - 1], rstd)
             if before:
-                finish(s - 1, residuals, centred_of[s - 1], rstd)
+                for i in range(0 if ahead else 1, PAIR):
+                    finish(s - 1, i, residuals, centred_of[s - 1], rstd)
 
             square_sum = stage2.tile([P, PAIR], F32)
             if current:

@@ -20,7 +20,7 @@ EDGE_PASSES = EDGES // K_PASS
 EDGE_TILES = EDGES // P
 QUARTERS = EDGES // (2 * P)
 LN_EPS = 1e-5
-VECTOR_RUNS = 16
+VECTOR_RUNS = 14
 LOAD_AHEAD = 3
 PAIR = 2
 PAIRS = NODES // (PAIR * P)
@@ -205,7 +205,7 @@ def tile_hgnnmodel_pa_t_kernel(tc, e_nodes, adj, ego_embeddings, ln_gamma, ln_be
         m_scales = resident.tile([P, EDGE_PASSES, EMB], U8, align_bytes=64)
 
         def empty_m_bank(t):
-            copy = nc.vector.tensor_copy if t in (0, 1, 7) else nc.scalar.copy
+            copy = nc.vector.tensor_copy if t in (1, 3, 5) else nc.scalar.copy
             copy(out=m_bf16[:, t, :], in_=m_banks[t][:])
 
         def regroup_m(k):

from contextlib import ExitStack

import concourse.mybir as mybir
from concourse.masks import make_identity

BF16 = mybir.dt.bfloat16
F32 = mybir.dt.float32
U32 = mybir.dt.uint32
U8 = mybir.dt.uint8
FP8X4 = mybir.dt.float8_e4m3fn_x4
ALU = mybir.AluOpType
ACT = mybir.ActivationFunctionType

P = 128
PACK = 4
K_PASS = P * PACK
NODES, EDGES, EMB = 4096, 1024, 512
GROUPS = NODES // K_PASS
EDGE_PASSES = EDGES // K_PASS
EDGE_TILES = EDGES // P
QUARTERS = EDGES // (2 * P)
LN_EPS = 1e-5
VECTOR_RUNS = 14
LOAD_AHEAD = 3
PAIR = 2
PAIRS = NODES // (PAIR * P)
LEAD = 3

FLOPS = 2 * 2 * NODES * EDGES * EMB


def tile_hgnnmodel_pa_t_kernel(tc, e_nodes, adj, ego_embeddings, ln_gamma, ln_beta, out):
    nc = tc.nc

    def node_rows(dram, g):
        return dram[g * K_PASS : (g + 1) * K_PASS, :].rearrange("(p j) c -> p (j c)", j=PACK)

    with ExitStack() as ctx:
        ctx.enter_context(tc.manual_schedule())
        consts = ctx.enter_context(tc.tile_pool(name="consts", bufs=1))
        resident = ctx.enter_context(tc.tile_pool(name="resident", bufs=1))
        results = ctx.enter_context(tc.tile_pool(name="results", bufs=4))
        psum = ctx.enter_context(tc.psum_pool(name="psum", bufs=1))
        tag_banks = {"sums": 3, "turned": 2, "residual": 3}

        def bank(tag, name="bank"):
            return psum.tile([P, EMB], F32, tag=tag, bufs=tag_banks[tag], name=name)

        identity = consts.tile([P, P], F32)
        make_identity(nc, identity[:])
        identity_bf16 = consts.tile([P, P], BF16)
        nc.gpsimd.tensor_copy(out=identity_bf16[:], in_=identity[:])

        ones = consts.tile([P, P], BF16)
        nc.vector.memset(ones[:], 1.0)
        table_warmer = consts.tile([P, 1], F32)
        nc.scalar.activation(out=table_warmer[:], in_=ones[:, 0:1], func=ACT.Abs_reciprocal_sqrt)
        beta_row = consts.tile([P, EMB], BF16)
        nc.vector.memset(beta_row[:], 0.0)
        nc.scalar.dma_start(out=beta_row[0:1, :], in_=ln_beta.unsqueeze(0))
        gamma_all = consts.tile([P, EMB], BF16)

        adj_rows = []

        def adj_pieces(g):
            return 2 if g == 0 else 1

        e_rows = []
        adj_grouped = []
        e_grouped = []
        m_bf16 = resident.tile([P, EDGE_TILES, EMB], BF16)

        with tc.tile_pool(name="stage1_rows", bufs=LOAD_AHEAD + 1) as rows_pool, tc.tile_pool(
            name="stage1", bufs=3
        ) as stage1, tc.tile_pool(name="stage1_codes", bufs=2) as stage1_codes:

            def load_group(g):
                e_tile = rows_pool.tile([P, PACK * EMB], BF16, name="e_rows")
                nc.sync.dma_start(out=e_tile[:], in_=node_rows(e_nodes, g))
                e_rows.append(e_tile)
                adj_tile = resident.tile([P, PACK * EDGES], BF16, name="adj_rows%d" % g)
                pieces = adj_pieces(g)
                for b in range(pieces):
                    nc.sync.dma_start(
                        out=adj_tile[:].rearrange("p (b j c) -> p b j c", b=pieces, j=PACK)[:, b],
                        in_=node_rows(adj, g).rearrange("p (j b c) -> p b j c", b=pieces, j=PACK)[:, b],
                    )
                adj_rows.append(adj_tile)

            def regroup(g):
                adj_tile = stage1.tile([P, EDGES, PACK], BF16, align_bytes=64, name="adj_grouped")
                pieces = adj_pieces(g)
                dst = adj_tile[:].rearrange("p (b a s c i) j -> p b s a c j i", b=pieces, a=QUARTERS // pieces, s=2, i=4)
                src = adj_rows[g][:].rearrange(
                    "p (b j a c i s) -> p b s a c j i", b=pieces, j=PACK, a=QUARTERS // pieces, i=4, s=2
                )
                e_tile = stage1.tile([P, EMB, PACK], BF16, align_bytes=64, name="e_grouped")
                nc.scalar.copy(
                    out=e_tile[:].rearrange("p (c i) j -> p c j i", i=4),
                    in_=e_rows[g][:].rearrange("p (j c i) -> p c j i", j=PACK, i=4),
                )
                for b in range(pieces):
                    nc.vector.tensor_copy(out=dst[:, b, 0], in_=src[:, b, 0])
                    nc.vector.tensor_copy(out=dst[:, b, 1, :, :VECTOR_RUNS], in_=src[:, b, 1, :, :VECTOR_RUNS])
                    nc.scalar.copy(out=dst[:, b, 1, :, VECTOR_RUNS:], in_=src[:, b, 1, :, VECTOR_RUNS:])
                adj_grouped.append(adj_tile)
                e_grouped.append(e_tile)

            codes_of = []

            def quantise(g):
                e_codes = stage1_codes.tile([P, EMB], U32, align_bytes=64)
                e_scales = stage1_codes.tile([P, EMB], U8, align_bytes=64)
                nc.vector.quantize_mx(
                    out=e_codes[:].bitcast(FP8X4),
                    scales=e_scales[:],
                    in_=e_grouped[g][:].rearrange("p w j -> p (w j)"),
                )
                adj_codes = stage1_codes.tile([P, EDGES], U32, align_bytes=64)
                adj_scales = stage1_codes.tile([P, EDGES], U8, align_bytes=64)
                pieces = 2 if g == GROUPS - 1 else 1
                for b in range(pieces):
                    cols = slice(b * EDGES // pieces, (b + 1) * EDGES // pieces)
                    nc.vector.quantize_mx(
                        out=adj_codes[:, cols].bitcast(FP8X4),
                        scales=adj_scales[:, cols],
                        in_=adj_grouped[g][:, cols].rearrange("p w j -> p (w j)"),
                    )
                codes_of.append((adj_codes, adj_scales, e_codes, e_scales))

            def multiply(g):
                adj_codes, adj_scales, e_codes, e_scales = codes_of[g]
                for t in range(EDGE_TILES):
                    nc.tensor.matmul_mx(
                        out=m_banks[t][:],
                        lhsT=adj_codes[:, t * P : (t + 1) * P].bitcast(FP8X4),
                        lhsT_scale=adj_scales[:, t * P : (t + 1) * P],
                        rhs=e_codes[:].bitcast(FP8X4),
                        rhs_scale=e_scales[:],
                        start=(g == 0),
                        stop=(g == GROUPS - 1),
                    )

            for g in range(LOAD_AHEAD):
                load_group(g)
            m_tags = ("turned", "turned", "sums", "sums", "sums", "residual", "residual", "residual")
            m_banks = [bank(m_tags[t], name="m_bank%d" % t) for t in range(EDGE_TILES)]
            for g in range(GROUPS):
                if g + LOAD_AHEAD < GROUPS:
                    load_group(g + LOAD_AHEAD)
                regroup(g)
                quantise(g)
                multiply(g)

            ego_rows = []
            for g in range(GROUPS):
                ego_tile = resident.tile([P, PACK, EMB], BF16, name="ego_rows%d" % g)
                nc.sync.dma_start(
                    out=ego_tile[:].rearrange("p j f -> p (j f)"), in_=node_rows(ego_embeddings, g)
                )
                ego_rows.append(ego_tile)
                if g == 1:
                    nc.sync.dma_start(out=gamma_all[:], in_=ln_gamma.partition_broadcast(P))

        stage2 = ctx.enter_context(tc.tile_pool(name="stage2", bufs=3))
        codes_pool = ctx.enter_context(tc.tile_pool(name="stage2_codes", bufs=LEAD + 2))
        turned_banks = []
        turned_words = []
        adjT_codes = []
        adjT_scales = []

        def transpose(s):
            g = s * PAIR // PACK
            pieces = adj_pieces(g)
            words = adj_rows[g][:].bitcast(F32).rearrange(
                "p (b j c q) -> p b c j q", b=pieces, j=PACK, q=P
            )
            for i in range(PAIR):
                j = (s * PAIR + i) % PACK
                turned = bank("turned")
                for c in range(2 * EDGE_PASSES):
                    b, rest = divmod(c, 2 * EDGE_PASSES // pieces)
                    nc.tensor.transpose(turned[:, c * P : (c + 1) * P], words[:, b, rest, j], identity[:])
                turned_banks.append(turned)
            grouped = stage2.tile([P, EDGE_PASSES * PAIR * P * PACK], BF16, align_bytes=64, name="adjT_grouped", bufs=LEAD)
            turned_words.append(grouped)

        def empty_turned(s, i):
            nc.scalar.copy(
                out=turned_words[s][:].bitcast(F32).rearrange(
                    "p (k j r u) -> p k j r u", k=EDGE_PASSES, j=PAIR, r=P, u=2
                )[:, :, i],
                in_=turned_banks[s * PAIR + i][:].rearrange("p (k u r) -> p k r u", k=EDGE_PASSES, u=2),
            )

        def quantise_turned(s):
            codes = codes_pool.tile([P, EDGE_PASSES * PAIR * P], U32, align_bytes=64, name="adjT_codes")
            scales = codes_pool.tile([P, EDGE_PASSES * PAIR * P], U8, align_bytes=64, name="adjT_scales")
            nc.vector.quantize_mx(out=codes[:].bitcast(FP8X4), scales=scales[:], in_=turned_words[s][:])
            adjT_codes.append(codes)
            adjT_scales.append(scales)

        m_grouped = resident.tile([P, EDGE_PASSES, EMB, PACK], BF16, align_bytes=64)
        m_codes = resident.tile([P, EDGE_PASSES, EMB], U32, align_bytes=64)
        m_scales = resident.tile([P, EDGE_PASSES, EMB], U8, align_bytes=64)

        def empty_m_bank(t):
            copy = nc.vector.tensor_copy if t in (1, 3, 5) else nc.scalar.copy
            copy(out=m_bf16[:, t, :], in_=m_banks[t][:])

        def regroup_m(k):
            nc.vector.tensor_copy(
                out=m_grouped[:, k].rearrange("p (c i) t -> p c t i", i=4),
                in_=m_bf16[:, k * PACK : (k + 1) * PACK, :].rearrange("p t (c i) -> p c t i", i=4),
            )

        def quantise_m(k):
            nc.vector.quantize_mx(
                out=m_codes[:, k, :].bitcast(FP8X4),
                scales=m_scales[:, k, :],
                in_=m_grouped[:, k].rearrange("p f t -> p (f t)"),
            )

        for t in range(PACK):
            empty_m_bank(t)
        regroup_m(0)
        for t in range(PACK, EDGE_TILES):
            empty_m_bank(t)
        quantise_m(0)
        regroup_m(1)
        for s in range(LEAD):
            transpose(s)
            for i in range(PAIR):
                empty_turned(s, i)
            quantise_turned(s)
            if s == 0:
                quantise_m(1)
        turned_beta = consts.tile([P, EMB], F32)
        beta_bank = bank("residual")
        for c in range(EMB // P):
            cols = slice(c * P, (c + 1) * P)
            nc.tensor.matmul(
                out=beta_bank[:, cols], lhsT=beta_row[:, cols], rhs=ones[:], start=True, stop=True
            )
        nc.scalar.copy(out=turned_beta[:], in_=beta_bank[:])

        def residual(s):
            tiles = []
            for i in range(PAIR):
                g, j = divmod(s * PAIR + i, PACK)
                added = bank("residual")
                nc.tensor.matmul(
                    out=added[:], lhsT=identity_bf16[:], rhs=ego_rows[g][:, j, :], start=True, stop=False
                )
                if i == 0:
                    nc.tensor.matmul(out=added[:], lhsT=ones[:], rhs=beta_row[:], start=False, stop=True)
                tiles.append(added)
            for c in range(EMB // P):
                cols = slice(c * P, (c + 1) * P)
                nc.tensor.matmul(
                    out=tiles[1][:, cols],
                    lhsT=turned_beta[:, cols],
                    rhs=identity[:],
                    start=False,
                    stop=(c == EMB // P - 1),
                    is_transpose=True,
                )
            return tiles

        def on_vector(s, i):
            return i == 1 and s % 3 == 0

        def finish(s, i, residuals, centred, rstd):
            g, j = divmod(s * PAIR + i, PACK)
            result = results.tile([P, EMB], F32)
            nc.vector.scalar_tensor_tensor(
                out=result[:],
                in0=centred[:, i, :],
                scalar=rstd[:, i : i + 1],
                in1=residuals[i][:],
                op0=ALU.mult,
                op1=ALU.add,
            )
            nc.sync.dma_start(out=node_rows(out, g)[:, j * EMB : (j + 1) * EMB], in_=result[:])

        def multiply_turned(s):
            h_banks = []
            for i in range(PAIR):
                h_bank = bank("sums")
                for k in range(EDGE_PASSES):
                    cols = slice((k * PAIR + i) * P, (k * PAIR + i + 1) * P)
                    nc.tensor.matmul_mx(
                        out=h_bank[:],
                        lhsT=adjT_codes[s][:, cols].bitcast(FP8X4),
                        lhsT_scale=adjT_scales[s][:, cols],
                        rhs=m_codes[:, k, :].bitcast(FP8X4),
                        rhs_scale=m_scales[:, k, :],
                        start=(k == 0),
                        stop=(k == EDGE_PASSES - 1),
                    )
                h_banks.append(h_bank)
            return h_banks

        next_banks = multiply_turned(0)
        centred_of = []
        square_sums = []
        moments_of = []
        for s in range(PAIRS + 1):
            current = s < PAIRS
            before = s > 0
            ahead = s + LEAD < PAIRS
            on_scalar = slice(0, 1) if on_vector(s, 1) else slice(0, PAIR)
            on_scalar_before = slice(0, 1) if on_vector(s - 1, 1) else slice(0, PAIR)

            if ahead:
                transpose(s + LEAD)
            h_banks = next_banks
            if s + 1 < PAIRS:
                next_banks = multiply_turned(s + 1)
            if before:
                residuals = residual(s - 1)

            h = stage2.tile([P, PAIR, EMB], F32)
            row_sum = stage2.tile([P, PAIR], F32)
            neg_mean = stage2.tile([P, PAIR], F32)
            stats = stage2.tile([P, 6], F32)
            moments = stage2.tile([P, 2], F32)
            if current:
                for i in range(PAIR):
                    if on_vector(s, i):
                        nc.vector.bn_stats(out=stats[:], in_=h_banks[i][:])
                    else:
                        nc.scalar.activation(
                            out=h[:, i, :], in_=h_banks[i][:], func=ACT.Identity, accum_out=row_sum[:, i : i + 1]
                        )
            if ahead:
                empty_turned(s + LEAD, 0)
            if current:
                nc.scalar.mul(out=neg_mean[:, on_scalar], in_=row_sum[:, on_scalar], mul=-1.0 / EMB)
            if ahead:
                empty_turned(s + LEAD, 1)
            if before:
                rstd = stage2.tile([P, PAIR], F32)
                nc.scalar.activation(
                    out=rstd[:, on_scalar_before],
                    in_=square_sums[s - 1][:, on_scalar_before],
                    func=ACT.Abs_reciprocal_sqrt,
                    bias=LN_EPS,
                    scale=1.0 / EMB,
                )
                if on_vector(s - 1, 1):
                    nc.scalar.activation(
                        out=rstd[:, 1:2],
                        in_=moments_of[s - 1][:, 1:2],
                        func=ACT.Abs_reciprocal_sqrt,
                        bias=LN_EPS,
                    )

            centred = stage2.tile([P, PAIR, EMB], F32)
            for i in range(PAIR):
                if current:
                    vector = on_vector(s, i)
                    nc.vector.scalar_tensor_tensor(
                        out=centred[:, i, :],
                        in0=h_banks[i][:] if vector else h[:, i, :],
                        scalar=moments[:, 0:1] if vector else neg_mean[:, i : i + 1],
                        in1=gamma_all[:],
                        op0=ALU.subtract if vector else ALU.add,
                        op1=ALU.mult,
                    )
                if i == 0:
                    if current and on_vector(s, 1):
                        nc.vector.bn_aggr(out=moments[:], in_=stats[:])
                    if ahead:
                        quantise_turned(s + LEAD)
                    elif before:
                        finish(s - 1, 0, residuals, centred_of[s - 1], rstd)
            if before:
                for i in range(0 if ahead else 1, PAIR):
                    finish(s - 1, i, residuals, centred_of[s - 1], rstd)

            square_sum = stage2.tile([P, PAIR], F32)
            if current:
                for i in range(PAIR):
                    if not on_vector(s, i):
                        squares = stage2.tile([P, EMB], BF16)
                        nc.scalar.activation(
                            out=squares[:],
                            in_=h[:, i, :],
                            func=ACT.Square,
                            bias=neg_mean[:, i : i + 1],
                            accum_out=square_sum[:, i : i + 1],
                        )
            centred_of.append(centred)
            square_sums.append(square_sum)
            moments_of.append(moments)
